import numpy as np
import ml_dtypes


def mxq(x, axis, fmt="e4m3"):
    dtype, down = {"e4m3": (ml_dtypes.float8_e4m3fn, 7), "e5m2": (ml_dtypes.float8_e5m2, 14)}[fmt]
    v = np.moveaxis(np.asarray(x, np.float32).astype(ml_dtypes.bfloat16).astype(np.float64), axis, -1)
    blocks = v.reshape(v.shape[:-1] + (-1, 32))
    amax = np.abs(blocks).max(-1, keepdims=True)
    byte = np.maximum(np.where(amax > 0, np.frexp(amax)[1] - 1 + 127, 0) - down, 1)
    scale = np.exp2(byte - 127.0)
    codes = (blocks / scale).astype(np.float32).astype(dtype).astype(np.float64)
    return np.moveaxis((codes * scale).reshape(v.shape), -1, axis)


WIDE = False


def mx_kscale(k):
    if not WIDE:
        return np.ones(k)
    levels = np.array([10, -10, 5, -5, 0])
    a = np.random.permutation(np.resize(levels, k // 512 * 4)).reshape(k // 512, 4)
    idx = np.arange(k)
    return np.exp2(a[idx // 512, idx % 128 // 32])


BF16 = ml_dtypes.bfloat16


def bf(x):
    return np.asarray(x, np.float32).astype(BF16)


def f64(x):
    return np.asarray(x).astype(np.float64)


E2M1 = np.array([0.0, 0.5, 1.0, 1.5, 2.0, 3.0, 4.0, 6.0, -0.0, -0.5, -1.0, -1.5, -2.0, -3.0, -4.0, -6.0])


def pack_weight(w, fmt):
    k, n = w.shape
    w = f64(bf(w)).reshape(k // 32, 32, n)
    amax = np.abs(w).max(1)
    if fmt == "e4m3":
        byte = np.frexp(amax)[1] - 1 + 127 - 7
    else:
        mant, ex = np.frexp(amax / 6.0)
        byte = np.where(mant > 0.5, ex, ex - 1) + 127
    byte = np.clip(np.where(amax > 0, byte, 1), 1, 254)
    scaled = (w * np.exp2(127.0 - byte)[:, None, :]).reshape(k, n).astype(np.float32)
    by_word = np.ascontiguousarray(scaled.reshape(k // 512, 128, 4, n).transpose(0, 1, 3, 2))
    if fmt == "e4m3":
        words = by_word.astype(ml_dtypes.float8_e4m3fn).view(np.uint8)
    else:
        c = by_word.astype(ml_dtypes.float4_e2m1fn).view(np.uint8) & 0xF
        words = c[..., 0::2] | (c[..., 1::2] << 4)
    return np.ascontiguousarray(words), np.ascontiguousarray(byte.astype(np.uint8).reshape(k // 512, 16, n))


def unpack_weight(words, scales, fmt):
    g, p, n, _ = words.shape
    if fmt == "e4m3":
        vals = np.ascontiguousarray(words).view(ml_dtypes.float8_e4m3fn).astype(np.float64)
    else:
        nib = np.empty((g, p, n, 4), np.uint8)
        nib[..., 0::2] = words & 0xF
        nib[..., 1::2] = words >> 4
        vals = E2M1[nib]
    vals = vals * np.repeat(np.exp2(scales.astype(np.float64) - 127.0), 8, axis=1)[..., None]
    return vals.transpose(0, 1, 3, 2).reshape(g * 512, n)


NTR, NTE, D, C = 2048, 256, 8192, 128
GAMMA = 10.0


def setup_inputs():
    s = mx_kscale(D)
    sM_words, sM_scales = pack_weight((np.random.standard_normal((NTR, D)) * s).T, "e4m3")
    x_test = bf(np.random.standard_normal((NTE, D)) / s)
    s_norm2 = bf(np.random.standard_normal(NTR) * np.sqrt(D))
    c_norm2 = bf(np.random.standard_normal(NTE) * np.sqrt(D))
    y_train_words, y_train_scales = pack_weight(np.random.standard_normal((NTR, C)) * 0.125 * np.sqrt(NTR), "e4m3")
    return {"sM_words": sM_words,
            "sM_scales": sM_scales,
            "x_test": x_test,
            "s_norm2": s_norm2,
            "c_norm2": c_norm2,
            "y_train_words": y_train_words,
            "y_train_scales": y_train_scales}


def reference(sM_words, sM_scales, x_test, s_norm2, c_norm2, y_train_words, y_train_scales):
    cross = unpack_weight(sM_words, sM_scales, "e4m3").T @ mxq(f64(x_test).T, 0, "e4m3")
    d2 = (-2.0) * cross + f64(s_norm2)[:, None] + f64(c_norm2)[None, :]
    dist = np.sqrt(np.clip(d2, 0.0, None))
    K = np.exp(dist * (-1.0 / GAMMA))
    Kt = K.T
    normalized = Kt / Kt.sum(axis=1, keepdims=True)
    return mxq(normalized, 1, "e4m3") @ unpack_weight(y_train_words, y_train_scales, "e4m3")

@@ -1,0 +1,221 @@
+from contextlib import ExitStack
+
+import concourse.mybir as mybir
+from concourse.masks import make_identity
+
+F32 = mybir.dt.float32
+BF16 = mybir.dt.bfloat16
+I32 = mybir.dt.int32
+U32 = mybir.dt.uint32
+U8 = mybir.dt.uint8
+FP8X4 = mybir.dt.float8_e4m3fn_x4
+ALU = mybir.AluOpType
+ACT = mybir.ActivationFunctionType
+AXIS = mybir.AxisListType
+
+P = 128
+PACK = 4
+K_PASS = P * PACK
+NTR, NTE, D, C = 2048, 256, 8192, 128
+GAMMA = 10.0
+
+FEAT_PASSES = D // K_PASS
+TEST_TILES = NTE // P
+ROUND = 512
+ROUNDS = NTR // ROUND
+GROUP = 4
+GROUPS = FEAT_PASSES // GROUP
+CHUNK = 2
+QUADRANT = 32
+SCALE_ROWS = 4
+
+FLOPS = 2 * NTR * D * NTE + 2 * NTE * NTR * C
+
+
+def tile_rbfnet_pb_k_kernel(
+    tc, sM_words, sM_scales, x_test, s_norm2, c_norm2, y_train_words, y_train_scales, out
+):
+    nc = tc.nc
+    with ExitStack() as stack:
+        keep = stack.enter_context(tc.tile_pool(name="keep", bufs=1))
+        xstage = stack.enter_context(tc.tile_pool(name="xstage", bufs=2))
+        stream = stack.enter_context(tc.tile_pool(name="stream", bufs=16))
+        work = stack.enter_context(tc.tile_pool(name="work", bufs=4))
+        psum = stack.enter_context(tc.psum_pool(name="psum", bufs=8))
+
+        ident_f32 = keep.tile([P, P], F32)
+        make_identity(nc, ident_f32[:])
+        ident_bf16 = keep.tile([P, P], BF16)
+        make_identity(nc, ident_bf16[:])
+        ones = keep.tile([P, P], BF16)
+        nc.vector.memset(ones[:], 1.0)
+
+        s_row = keep.tile([P, NTR], BF16)
+        nc.vector.memset(s_row[:], 0.0)
+        nc.scalar.dma_start(out=s_row[0:1, :], in_=s_norm2.rearrange("(o n) -> o n", o=1))
+
+        c_bf16 = keep.tile([P, TEST_TILES], BF16)
+        with nc.allow_non_contiguous_dma(reason="256 two-byte values, one to a partition"):
+            nc.scalar.dma_start(out=c_bf16[:], in_=c_norm2.rearrange("(a p) -> p a", p=P))
+        c_col = keep.tile([P, TEST_TILES], F32)
+        nc.vector.tensor_copy(out=c_col[:], in_=c_bf16[:])
+
+        x_raw = keep.tile([P, TEST_TILES, D], BF16)
+        for kc in range(GROUPS):
+            cols = slice(kc * GROUP * K_PASS, (kc + 1) * GROUP * K_PASS)
+            for jt in range(TEST_TILES):
+                nc.sync.dma_start(out=x_raw[:, jt, cols], in_=x_test[jt * P : (jt + 1) * P, cols])
+
+        sm_planes = keep.tile([P, GROUPS, NTR], U8, align_bytes=64)
+        nc.vector.memset(sm_planes[:].bitcast(I32), 0)
+        y_planes = keep.tile([P, C], U8, align_bytes=64)
+        nc.vector.memset(y_planes[:].bitcast(I32), 0)
+        live = GROUP * SCALE_ROWS
+        for a in range(GROUPS):
+            for quad in range(P // QUADRANT):
+                nc.sync.dma_start(
+                    out=sm_planes[quad * QUADRANT : quad * QUADRANT + live, a, :].bitcast(I32),
+                    in_=sM_scales[
+                        a * GROUP : (a + 1) * GROUP, quad * SCALE_ROWS : (quad + 1) * SCALE_ROWS, :
+                    ].bitcast(I32),
+                )
+        for quad in range(P // QUADRANT):
+            nc.sync.dma_start(
+                out=y_planes[quad * QUADRANT : quad * QUADRANT + live, :].bitcast(I32),
+                in_=y_train_scales[:, quad * SCALE_ROWS : (quad + 1) * SCALE_ROWS, :].bitcast(I32),
+            )
+        y_codes = keep.tile([P, ROUNDS, C], I32, align_bytes=64)
+        nc.sync.dma_start(
+            out=y_codes[:], in_=y_train_words.rearrange("g p n t -> p g (n t)").bitcast(I32)
+        )
+
+        x_words = x_raw[:].bitcast(F32)
+        x_codes = keep.tile([P, FEAT_PASSES, NTE], U32, align_bytes=64)
+        x_planes = keep.tile([P, FEAT_PASSES, NTE], U8, align_bytes=64)
+        half = K_PASS // 2
+        for kc in range(GROUPS):
+            grouped = xstage.tile([P, GROUP, TEST_TILES, P, PACK], BF16, align_bytes=64)
+            grouped_words = grouped[:].bitcast(F32)
+            for gi in range(GROUP):
+                g = kc * GROUP + gi
+                xt = psum.tile([P, TEST_TILES, 2, P], F32, tag="bank")
+                for jt in range(TEST_TILES):
+                    for u in range(2):
+                        nc.tensor.transpose(
+                            xt[:, jt, u, :],
+                            x_words[:, jt, g * half + u : (g + 1) * half : 2],
+                            ident_f32[:],
+                        )
+                copy = nc.vector.tensor_copy if gi == GROUP - 1 else nc.scalar.copy
+                copy(out=grouped_words[:, gi], in_=xt[:].rearrange("p a u j -> p a j u"))
+            passes = slice(kc * GROUP, (kc + 1) * GROUP)
+            nc.vector.quantize_mx(
+                out=x_codes[:, passes, :].rearrange("p g j -> p (g j)").bitcast(FP8X4),
+                scales=x_planes[:, passes, :].rearrange("p g j -> p (g j)"),
+                in_=grouped[:].rearrange("p g a j t -> p (g a j t)"),
+            )
+
+        s_all = keep.tile([P, ROUNDS, PACK, P], BF16)
+        for r in range(ROUNDS):
+            s_bank = psum.tile([P, ROUND], F32, tag="bank")
+            nc.tensor.matmul(
+                out=s_bank[:], lhsT=ones[:], rhs=s_row[:, r * ROUND : (r + 1) * ROUND],
+                start=True, stop=True,
+            )
+            nc.vector.tensor_copy(
+                out=s_all[:, r], in_=s_bank[:].rearrange("p (q t) -> p t q", t=PACK)
+            )
+
+        kern = keep.tile([P, TEST_TILES, ROUNDS, PACK, P], F32)
+        ksum = keep.tile([P, TEST_TILES, ROUNDS], F32)
+        for r in range(ROUNDS):
+            acc = [
+                psum.tile([P, ROUND], F32, tag="bank", name="acc%d" % jt)
+                for jt in range(TEST_TILES)
+            ]
+            for first in range(0, FEAT_PASSES, CHUNK):
+                sm = stream.tile([P, CHUNK, ROUND], I32, align_bytes=64)
+                nc.sync.dma_start(
+                    out=sm[:],
+                    in_=sM_words[first : first + CHUNK, :, r * ROUND : (r + 1) * ROUND, :]
+                    .rearrange("g p n t -> p g (n t)")
+                    .bitcast(I32),
+                )
+                for i in range(CHUNK):
+                    g = first + i
+                    a, b = divmod(g, GROUP)
+                    for jt in range(TEST_TILES):
+                        nc.tensor.matmul_mx(
+                            out=acc[jt][:],
+                            lhsT=x_codes[:, g, jt * P : (jt + 1) * P].bitcast(FP8X4),
+                            lhsT_scale=x_planes[:, g, jt * P : (jt + 1) * P],
+                            rhs=sm[:, i, :].bitcast(FP8X4),
+                            rhs_scale=sm_planes[b * SCALE_ROWS : P, a, r * ROUND : (r + 1) * ROUND],
+                            start=(g == 0),
+                            stop=(g == FEAT_PASSES - 1),
+                        )
+            d2 = [work.tile([P, PACK, P], F32, tag="d2", name="d2_%d" % jt) for jt in range(TEST_TILES)]
+            for jt in range(TEST_TILES):
+                nc.vector.scalar_tensor_tensor(
+                    out=d2[jt][:],
+                    in0=acc[jt][:].rearrange("p (q t) -> p t q", t=PACK),
+                    scalar=-2.0,
+                    in1=s_all[:, r],
+                    op0=ALU.mult,
+                    op1=ALU.add,
+                )
+            clamped = [work.tile([P, PACK, P], F32, tag="clamped", name="clamped%d" % jt) for jt in range(TEST_TILES)]
+            for jt in range(TEST_TILES):
+                nc.vector.tensor_scalar(
+                    out=clamped[jt][:], in0=d2[jt][:], scalar1=c_col[:, jt : jt + 1], scalar2=0.0,
+                    op0=ALU.add, op1=ALU.max,
+                )
+            dist = [work.tile([P, PACK, P], F32, tag="dist", name="dist%d" % jt) for jt in range(TEST_TILES)]
+            for jt in range(TEST_TILES):
+                nc.scalar.activation(out=dist[jt][:], in_=clamped[jt][:], func=ACT.Sqrt)
+            for jt in range(TEST_TILES):
+                nc.scalar.activation(
+                    out=kern[:, jt, r], in_=dist[jt][:], func=ACT.Exp, scale=-1.0 / GAMMA,
+                    accum_out=ksum[:, jt, r : r + 1],
+                )
+
+        total = keep.tile([P, TEST_TILES], F32)
+        rsum = keep.tile([P, TEST_TILES], F32)
+        w_codes = keep.tile([P, TEST_TILES, ROUNDS, P], U32, align_bytes=64)
+        w_planes = keep.tile([P, TEST_TILES, ROUNDS, P], U8, align_bytes=64)
+        for jt in range(TEST_TILES):
+            nc.vector.tensor_reduce(
+                out=total[:, jt : jt + 1], in_=ksum[:, jt, :], axis=AXIS.X, op=ALU.add
+            )
+            nc.vector.reciprocal(out=rsum[:, jt : jt + 1], in_=total[:, jt : jt + 1])
+            for r in range(ROUNDS):
+                w_bf16 = work.tile([P, PACK, P], BF16)
+                nc.vector.tensor_scalar(
+                    out=w_bf16[:], in0=kern[:, jt, r], scalar1=rsum[:, jt : jt + 1], scalar2=None,
+                    op0=ALU.mult,
+                )
+                wt = psum.tile([P, PACK, P], BF16, tag="bank")
+                for t in range(PACK):
+                    nc.tensor.transpose(wt[:, t, :], w_bf16[:, t, :], ident_bf16[:])
+                w_grouped = work.tile([P, P, PACK], BF16, align_bytes=64)
+                nc.scalar.copy(out=w_grouped[:], in_=wt[:].rearrange("p t j -> p j t"))
+                nc.vector.quantize_mx(
+                    out=w_codes[:, jt, r, :].bitcast(FP8X4),
+                    scales=w_planes[:, jt, r, :],
+                    in_=w_grouped[:].rearrange("p j t -> p (j t)"),
+                )
+        for jt in range(TEST_TILES):
+            o_bank = psum.tile([P, C], F32, tag="bank")
+            for r in range(ROUNDS):
+                nc.tensor.matmul_mx(
+                    out=o_bank[:],
+                    lhsT=w_codes[:, jt, r, :].bitcast(FP8X4),
+                    lhsT_scale=w_planes[:, jt, r, :],
+                    rhs=y_codes[:, r, :].bitcast(FP8X4),
+                    rhs_scale=y_planes[r * SCALE_ROWS : P, :],
+                    start=(r == 0),
+                    stop=(r == ROUNDS - 1),
+                )
+            result = work.tile([P, C], F32)
+            nc.vector.tensor_copy(out=result[:], in_=o_bank[:])
+            nc.sync.dma_start(out=out[jt * P : (jt + 1) * P, :], in_=result[:])

@@ -21,13 +21,15 @@ GAMMA = 10.0
 
 FEAT_PASSES = D // K_PASS
 TEST_TILES = NTE // P
-ROUND = 512
-ROUNDS = NTR // ROUND
+BLOCK = 512
+BLOCKS = NTR // BLOCK
+ROUND_BLOCKS = ((0, 1), (2,), (3,))
 GROUP = 4
 GROUPS = FEAT_PASSES // GROUP
-CHUNK = 2
+STREAM_WORDS = 1024
 QUADRANT = 32
 SCALE_ROWS = 4
+QUAD_ORDER = (0, 2, 1, 3)
 
 FLOPS = 2 * NTR * D * NTE + 2 * NTE * NTR * C
 
@@ -72,22 +74,13 @@ def tile_rbfnet_pb_k_kernel(
         nc.vector.memset(y_planes[:].bitcast(I32), 0)
         live = GROUP * SCALE_ROWS
         for a in range(GROUPS):
-            for quad in range(P // QUADRANT):
+            for quad in QUAD_ORDER:
                 nc.sync.dma_start(
                     out=sm_planes[quad * QUADRANT : quad * QUADRANT + live, a, :].bitcast(I32),
                     in_=sM_scales[
                         a * GROUP : (a + 1) * GROUP, quad * SCALE_ROWS : (quad + 1) * SCALE_ROWS, :
                     ].bitcast(I32),
                 )
-        for quad in range(P // QUADRANT):
-            nc.sync.dma_start(
-                out=y_planes[quad * QUADRANT : quad * QUADRANT + live, :].bitcast(I32),
-                in_=y_train_scales[:, quad * SCALE_ROWS : (quad + 1) * SCALE_ROWS, :].bitcast(I32),
-            )
-        y_codes = keep.tile([P, ROUNDS, C], I32, align_bytes=64)
-        nc.sync.dma_start(
-            out=y_codes[:], in_=y_train_words.rearrange("g p n t -> p g (n t)").bitcast(I32)
-        )
 
         x_words = x_raw[:].bitcast(F32)
         x_codes = keep.tile([P, FEAT_PASSES, NTE], U32, align_bytes=64)
@@ -115,83 +108,100 @@ def tile_rbfnet_pb_k_kernel(
                 in_=grouped[:].rearrange("p g a j t -> p (g a j t)"),
             )
 
-        s_all = keep.tile([P, ROUNDS, PACK, P], BF16)
-        for r in range(ROUNDS):
-            s_bank = psum.tile([P, ROUND], F32, tag="bank")
+        s_all = keep.tile([P, BLOCKS, PACK, P], BF16)
+        for blk in range(BLOCKS):
+            s_bank = psum.tile([P, BLOCK], F32, tag="bank")
             nc.tensor.matmul(
-                out=s_bank[:], lhsT=ones[:], rhs=s_row[:, r * ROUND : (r + 1) * ROUND],
+                out=s_bank[:], lhsT=ones[:], rhs=s_row[:, blk * BLOCK : (blk + 1) * BLOCK],
                 start=True, stop=True,
             )
             nc.vector.tensor_copy(
-                out=s_all[:, r], in_=s_bank[:].rearrange("p (q t) -> p t q", t=PACK)
+                out=s_all[:, blk], in_=s_bank[:].rearrange("p (q t) -> p t q", t=PACK)
             )
 
-        kern = keep.tile([P, TEST_TILES, ROUNDS, PACK, P], F32)
-        ksum = keep.tile([P, TEST_TILES, ROUNDS], F32)
-        for r in range(ROUNDS):
-            acc = [
-                psum.tile([P, ROUND], F32, tag="bank", name="acc%d" % jt)
-                for jt in range(TEST_TILES)
-            ]
-            for first in range(0, FEAT_PASSES, CHUNK):
-                sm = stream.tile([P, CHUNK, ROUND], I32, align_bytes=64)
+        kern = keep.tile([P, TEST_TILES, BLOCKS, PACK, P], F32)
+        ksum = keep.tile([P, TEST_TILES, BLOCKS], F32)
+        for blocks in ROUND_BLOCKS:
+            units = [(jt, blk) for jt in range(TEST_TILES) for blk in blocks]
+            first_col = blocks[0] * BLOCK
+            width = len(blocks) * BLOCK
+            chunk = STREAM_WORDS // width
+            acc = {}
+            for jt, blk in units:
+                acc[jt, blk] = psum.tile([P, BLOCK], F32, tag="bank", name="acc_%d_%d" % (jt, blk))
+            for first in range(0, FEAT_PASSES, chunk):
+                sm = stream.tile([P, chunk, width], I32, align_bytes=64, tag="sm")
                 nc.sync.dma_start(
                     out=sm[:],
-                    in_=sM_words[first : first + CHUNK, :, r * ROUND : (r + 1) * ROUND, :]
+                    in_=sM_words[first : first + chunk, :, first_col : first_col + width, :]
                     .rearrange("g p n t -> p g (n t)")
                     .bitcast(I32),
                 )
-                for i in range(CHUNK):
+                for i in range(chunk):
                     g = first + i
                     a, b = divmod(g, GROUP)
-                    for jt in range(TEST_TILES):
+                    for jt, blk in units:
+                        local = (blk - blocks[0]) * BLOCK
                         nc.tensor.matmul_mx(
-                            out=acc[jt][:],
+                            out=acc[jt, blk][:],
                             lhsT=x_codes[:, g, jt * P : (jt + 1) * P].bitcast(FP8X4),
                             lhsT_scale=x_planes[:, g, jt * P : (jt + 1) * P],
-                            rhs=sm[:, i, :].bitcast(FP8X4),
-                            rhs_scale=sm_planes[b * SCALE_ROWS : P, a, r * ROUND : (r + 1) * ROUND],
+                            rhs=sm[:, i, local : local + BLOCK].bitcast(FP8X4),
+                            rhs_scale=sm_planes[b * SCALE_ROWS : P, a, blk * BLOCK : (blk + 1) * BLOCK],
                             start=(g == 0),
                             stop=(g == FEAT_PASSES - 1),
                         )
-            d2 = [work.tile([P, PACK, P], F32, tag="d2", name="d2_%d" % jt) for jt in range(TEST_TILES)]
-            for jt in range(TEST_TILES):
+            d2, clamped, dist = {}, {}, {}
+            for jt, blk in units:
+                d2[jt, blk] = work.tile([P, PACK, P], F32, tag="d2", name="d2_%d_%d" % (jt, blk))
                 nc.vector.scalar_tensor_tensor(
-                    out=d2[jt][:],
-                    in0=acc[jt][:].rearrange("p (q t) -> p t q", t=PACK),
+                    out=d2[jt, blk][:],
+                    in0=acc[jt, blk][:].rearrange("p (q t) -> p t q", t=PACK),
                     scalar=-2.0,
-                    in1=s_all[:, r],
+                    in1=s_all[:, blk],
                     op0=ALU.mult,
                     op1=ALU.add,
                 )
-            clamped = [work.tile([P, PACK, P], F32, tag="clamped", name="clamped%d" % jt) for jt in range(TEST_TILES)]
-            for jt in range(TEST_TILES):
+            for jt, blk in units:
+                clamped[jt, blk] = work.tile(
+                    [P, PACK, P], F32, tag="clamped", name="clamped_%d_%d" % (jt, blk)
+                )
                 nc.vector.tensor_scalar(
-                    out=clamped[jt][:], in0=d2[jt][:], scalar1=c_col[:, jt : jt + 1], scalar2=0.0,
-                    op0=ALU.add, op1=ALU.max,
+                    out=clamped[jt, blk][:], in0=d2[jt, blk][:],
+                    scalar1=c_col[:, jt : jt + 1], scalar2=0.0, op0=ALU.add, op1=ALU.max,
                 )
-            dist = [work.tile([P, PACK, P], F32, tag="dist", name="dist%d" % jt) for jt in range(TEST_TILES)]
-            for jt in range(TEST_TILES):
-                nc.scalar.activation(out=dist[jt][:], in_=clamped[jt][:], func=ACT.Sqrt)
-            for jt in range(TEST_TILES):
+            for jt, blk in units:
+                dist[jt, blk] = work.tile([P, PACK, P], F32, tag="dist", name="dist_%d_%d" % (jt, blk))
+                nc.scalar.activation(out=dist[jt, blk][:], in_=clamped[jt, blk][:], func=ACT.Sqrt)
+            for jt, blk in units:
                 nc.scalar.activation(
-                    out=kern[:, jt, r], in_=dist[jt][:], func=ACT.Exp, scale=-1.0 / GAMMA,
-                    accum_out=ksum[:, jt, r : r + 1],
+                    out=kern[:, jt, blk], in_=dist[jt, blk][:], func=ACT.Exp, scale=-1.0 / GAMMA,
+                    accum_out=ksum[:, jt, blk : blk + 1],
                 )
+
+        for quad in QUAD_ORDER:
+            nc.sync.dma_start(
+                out=y_planes[quad * QUADRANT : quad * QUADRANT + live, :].bitcast(I32),
+                in_=y_train_scales[:, quad * SCALE_ROWS : (quad + 1) * SCALE_ROWS, :].bitcast(I32),
+            )
+        y_codes = keep.tile([P, BLOCKS, C], I32, align_bytes=64)
+        nc.sync.dma_start(
+            out=y_codes[:], in_=y_train_words.rearrange("g p n t -> p g (n t)").bitcast(I32)
+        )
 
         total = keep.tile([P, TEST_TILES], F32)
         rsum = keep.tile([P, TEST_TILES], F32)
-        w_codes = keep.tile([P, TEST_TILES, ROUNDS, P], U32, align_bytes=64)
-        w_planes = keep.tile([P, TEST_TILES, ROUNDS, P], U8, align_bytes=64)
+        w_codes = keep.tile([P, TEST_TILES, BLOCKS, P], U32, align_bytes=64)
+        w_planes = keep.tile([P, TEST_TILES, BLOCKS, P], U8, align_bytes=64)
         for jt in range(TEST_TILES):
             nc.vector.tensor_reduce(
                 out=total[:, jt : jt + 1], in_=ksum[:, jt, :], axis=AXIS.X, op=ALU.add
             )
             nc.vector.reciprocal(out=rsum[:, jt : jt + 1], in_=total[:, jt : jt + 1])
-            for r in range(ROUNDS):
+            for blk in range(BLOCKS):
                 w_bf16 = work.tile([P, PACK, P], BF16)
                 nc.vector.tensor_scalar(
-                    out=w_bf16[:], in0=kern[:, jt, r], scalar1=rsum[:, jt : jt + 1], scalar2=None,
+                    out=w_bf16[:], in0=kern[:, jt, blk], scalar1=rsum[:, jt : jt + 1], scalar2=None,
                     op0=ALU.mult,
                 )
                 wt = psum.tile([P, PACK, P], BF16, tag="bank")
@@ -200,21 +210,21 @@ def tile_rbfnet_pb_k_kernel(
                 w_grouped = work.tile([P, P, PACK], BF16, align_bytes=64)
                 nc.scalar.copy(out=w_grouped[:], in_=wt[:].rearrange("p t j -> p j t"))
                 nc.vector.quantize_mx(
-                    out=w_codes[:, jt, r, :].bitcast(FP8X4),
-                    scales=w_planes[:, jt, r, :],
+                    out=w_codes[:, jt, blk, :].bitcast(FP8X4),
+                    scales=w_planes[:, jt, blk, :],
                     in_=w_grouped[:].rearrange("p j t -> p (j t)"),
                 )
         for jt in range(TEST_TILES):
             o_bank = psum.tile([P, C], F32, tag="bank")
-            for r in range(ROUNDS):
+            for blk in range(BLOCKS):
                 nc.tensor.matmul_mx(
                     out=o_bank[:],
-                    lhsT=w_codes[:, jt, r, :].bitcast(FP8X4),
-                    lhsT_scale=w_planes[:, jt, r, :],
-                    rhs=y_codes[:, r, :].bitcast(FP8X4),
-                    rhs_scale=y_planes[r * SCALE_ROWS : P, :],
-                    start=(r == 0),
-                    stop=(r == ROUNDS - 1),
+                    lhsT=w_codes[:, jt, blk, :].bitcast(FP8X4),
+                    lhsT_scale=w_planes[:, jt, blk, :],
+                    rhs=y_codes[:, blk, :].bitcast(FP8X4),
+                    rhs_scale=y_planes[blk * SCALE_ROWS : P, :],
+                    start=(blk == 0),
+                    stop=(blk == BLOCKS - 1),
                 )
             result = work.tile([P, C], F32)
             nc.vector.tensor_copy(out=result[:], in_=o_bank[:])

@@ -23,13 +23,19 @@ FEAT_PASSES = D // K_PASS
 TEST_TILES = NTE // P
 BLOCK = 512
 BLOCKS = NTR // BLOCK
-ROUND_BLOCKS = ((0, 1), (2,), (3,))
+HALF = BLOCK // 2
 GROUP = 4
 GROUPS = FEAT_PASSES // GROUP
-STREAM_WORDS = 1024
 QUADRANT = 32
 SCALE_ROWS = 4
+LIVE = GROUP * SCALE_ROWS
 QUAD_ORDER = (0, 2, 1, 3)
+WIDE = 2
+STEP = 2
+STEPS = FEAT_PASSES // STEP
+SPLIT = 12
+LOOKAHEAD = 6
+WARM = 16
 
 FLOPS = 2 * NTR * D * NTE + 2 * NTE * NTR * C
 
@@ -40,192 +46,324 @@ def tile_rbfnet_pb_k_kernel(
     nc = tc.nc
     with ExitStack() as stack:
         keep = stack.enter_context(tc.tile_pool(name="keep", bufs=1))
-        xstage = stack.enter_context(tc.tile_pool(name="xstage", bufs=2))
-        stream = stack.enter_context(tc.tile_pool(name="stream", bufs=16))
+        xstage = stack.enter_context(tc.tile_pool(name="xstage", bufs=3))
+        stream = stack.enter_context(tc.tile_pool(name="stream", bufs=LOOKAHEAD + 2))
+        narrow = stack.enter_context(tc.tile_pool(name="narrow", bufs=14))
         work = stack.enter_context(tc.tile_pool(name="work", bufs=4))
-        psum = stack.enter_context(tc.psum_pool(name="psum", bufs=8))
+        psum_wide = stack.enter_context(tc.psum_pool(name="psum_wide", bufs=4))
+        psum_turn = stack.enter_context(tc.psum_pool(name="psum_turn", bufs=4))
+        stack.enter_context(tc.manual_schedule())
 
-        ident_f32 = keep.tile([P, P], F32)
-        make_identity(nc, ident_f32[:])
-        ident_bf16 = keep.tile([P, P], BF16)
-        make_identity(nc, ident_bf16[:])
-        ones = keep.tile([P, P], BF16)
-        nc.vector.memset(ones[:], 1.0)
+        sm_planes = []
+        for a in range(GROUPS):
+            plane = keep.tile([P, NTR], U8, align_bytes=64, name="sm_planes_%d" % a)
+            sm_planes.append(plane)
+        y_planes = keep.tile([P, C], U8, align_bytes=64)
 
+        def load_scales(queue, dtype, plane, source):
+            for quad in QUAD_ORDER:
+                queue.dma_start(
+                    out=plane[quad * QUADRANT : quad * QUADRANT + LIVE, :].bitcast(dtype),
+                    in_=source[:, quad * SCALE_ROWS : (quad + 1) * SCALE_ROWS, :].bitcast(dtype),
+                )
+
+        nc.vector.memset(sm_planes[0][:].bitcast(I32), 0)
         s_row = keep.tile([P, NTR], BF16)
-        nc.vector.memset(s_row[:], 0.0)
+        nc.gpsimd.memset(s_row[:].bitcast(I32), 0)
         nc.scalar.dma_start(out=s_row[0:1, :], in_=s_norm2.rearrange("(o n) -> o n", o=1))
-
         c_bf16 = keep.tile([P, TEST_TILES], BF16)
         with nc.allow_non_contiguous_dma(reason="256 two-byte values, one to a partition"):
             nc.scalar.dma_start(out=c_bf16[:], in_=c_norm2.rearrange("(a p) -> p a", p=P))
-        c_col = keep.tile([P, TEST_TILES], F32)
-        nc.vector.tensor_copy(out=c_col[:], in_=c_bf16[:])
+        ident_f32 = keep.tile([P, P], F32)
+        make_identity(nc, ident_f32[:])
+        ones = keep.tile([P, P], BF16)
+        nc.vector.memset(ones[:], 1.0)
+        for a in range(1, GROUPS):
+            nc.gpsimd.memset(sm_planes[a][:].bitcast(I32), 0)
+            load_scales(nc.gpsimd, F32, sm_planes[a], sM_scales[a * GROUP : (a + 1) * GROUP])
+        nc.gpsimd.memset(y_planes[:].bitcast(I32), 0)
+        ident_bf16 = keep.tile([P, P], BF16)
+        make_identity(nc, ident_bf16[:])
 
         x_raw = keep.tile([P, TEST_TILES, D], BF16)
-        for kc in range(GROUPS):
-            cols = slice(kc * GROUP * K_PASS, (kc + 1) * GROUP * K_PASS)
-            for jt in range(TEST_TILES):
-                nc.sync.dma_start(out=x_raw[:, jt, cols], in_=x_test[jt * P : (jt + 1) * P, cols])
+        sm_tiles = {}
+        order = [("x", 0, 2), ("s", 0, 0), ("m", 0, 1), ("x", 2, 2), ("m", 1, 1), ("x", 4, 4)]
+        order += [("m", g, 1) for g in range(2, 6)] + [("x", 8, 4)]
+        order += [("m", g, 1) for g in range(6, 10)] + [("x", 12, 4)]
+        order += [("m", g, 1) for g in range(10, FEAT_PASSES)]
 
-        sm_planes = keep.tile([P, GROUPS, NTR], U8, align_bytes=64)
-        nc.vector.memset(sm_planes[:].bitcast(I32), 0)
-        y_planes = keep.tile([P, C], U8, align_bytes=64)
-        nc.vector.memset(y_planes[:].bitcast(I32), 0)
-        live = GROUP * SCALE_ROWS
-        for a in range(GROUPS):
-            for quad in QUAD_ORDER:
-                nc.sync.dma_start(
-                    out=sm_planes[quad * QUADRANT : quad * QUADRANT + live, a, :].bitcast(I32),
-                    in_=sM_scales[
-                        a * GROUP : (a + 1) * GROUP, quad * SCALE_ROWS : (quad + 1) * SCALE_ROWS, :
-                    ].bitcast(I32),
-                )
+        def issue(last_pass):
+            while order and (order[0][0] != "m" or order[0][1] <= last_pass):
+                kind, first, count = order[0]
+                order.remove(order[0])
+                if kind == "s":
+                    load_scales(nc.sync, I32, sm_planes[0], sM_scales[:GROUP])
+                elif kind == "x":
+                    cols = slice(first * K_PASS, (first + count) * K_PASS)
+                    for jt in range(TEST_TILES):
+                        nc.sync.dma_start(
+                            out=x_raw[:, jt, cols], in_=x_test[jt * P : (jt + 1) * P, cols]
+                        )
+                else:
+                    sm_tiles[first] = stream.tile(
+                        [P, WIDE * BLOCK], I32, align_bytes=64, tag="sm", name="sm_%d" % first
+                    )
+                    nc.sync.dma_start(
+                        out=sm_tiles[first][:],
+                        in_=sM_words[first, :, : WIDE * BLOCK, :]
+                        .rearrange("p n t -> p (n t)")
+                        .bitcast(I32),
+                    )
 
         x_words = x_raw[:].bitcast(F32)
         x_codes = keep.tile([P, FEAT_PASSES, NTE], U32, align_bytes=64)
         x_planes = keep.tile([P, FEAT_PASSES, NTE], U8, align_bytes=64)
         half = K_PASS // 2
-        for kc in range(GROUPS):
-            grouped = xstage.tile([P, GROUP, TEST_TILES, P, PACK], BF16, align_bytes=64)
+        runs = {}
+
+        def reorder(step):
+            runs[step] = xstage.tile([P, TEST_TILES, STEP, 2, P], F32, tag="runs", name="runs")
+            for jt in range(TEST_TILES):
+                nc.vector.tensor_copy(
+                    out=runs[step][:, jt],
+                    in_=x_words[:, jt, step * STEP * half : (step + 1) * STEP * half].rearrange(
+                        "j (g p u) -> j g u p", g=STEP, u=2
+                    ),
+                )
+
+        def prepare(step):
+            grouped = xstage.tile([P, STEP, TEST_TILES, P, PACK], BF16, align_bytes=64, name="grouped")
             grouped_words = grouped[:].bitcast(F32)
-            for gi in range(GROUP):
-                g = kc * GROUP + gi
-                xt = psum.tile([P, TEST_TILES, 2, P], F32, tag="bank")
+            for i in range(STEP):
+                xt = psum_turn.tile([P, TEST_TILES, 2, P], F32, tag="turn", name="xt")
                 for jt in range(TEST_TILES):
                     for u in range(2):
-                        nc.tensor.transpose(
-                            xt[:, jt, u, :],
-                            x_words[:, jt, g * half + u : (g + 1) * half : 2],
-                            ident_f32[:],
-                        )
-                copy = nc.vector.tensor_copy if gi == GROUP - 1 else nc.scalar.copy
-                copy(out=grouped_words[:, gi], in_=xt[:].rearrange("p a u j -> p a j u"))
-            passes = slice(kc * GROUP, (kc + 1) * GROUP)
+                        nc.tensor.transpose(xt[:, jt, u, :], runs[step][:, jt, i, u, :], ident_f32[:])
+                copy = nc.vector.tensor_copy if i == STEP - 1 else nc.scalar.copy
+                copy(out=grouped_words[:, i], in_=xt[:].rearrange("p a u j -> p a j u"))
+            passes = slice(step * STEP, (step + 1) * STEP)
             nc.vector.quantize_mx(
                 out=x_codes[:, passes, :].rearrange("p g j -> p (g j)").bitcast(FP8X4),
                 scales=x_planes[:, passes, :].rearrange("p g j -> p (g j)"),
                 in_=grouped[:].rearrange("p g a j t -> p (g a j t)"),
             )
+            if step + 1 < STEPS:
+                reorder(step + 1)
 
+        kern = keep.tile([P, TEST_TILES, BLOCKS, PACK, P], F32)
+        ksum = keep.tile([P, TEST_TILES, BLOCKS + 1], F32)
         s_all = keep.tile([P, BLOCKS, PACK, P], BF16)
+        c_col = keep.tile([P, TEST_TILES], F32)
+        acc, d2 = {}, {}
+
+        def multiply(g, words, unit):
+            jt, n0, n = unit
+            a, b = divmod(g, GROUP)
+            nc.tensor.matmul_mx(
+                out=acc[unit][:],
+                lhsT=x_codes[:, g, jt * P : (jt + 1) * P].bitcast(FP8X4),
+                lhsT_scale=x_planes[:, g, jt * P : (jt + 1) * P],
+                rhs=words.bitcast(FP8X4),
+                rhs_scale=sm_planes[a][b * SCALE_ROWS : P, n0 : n0 + n],
+                start=(g == 0),
+                stop=(g == FEAT_PASSES - 1),
+            )
+
+        def place(tensor, unit):
+            jt, n0, n = unit
+            q0 = n0 % BLOCK // PACK
+            return tensor[:, :, q0 : q0 + n // PACK]
+
+        def squared_distance(unit):
+            jt, n0, n = unit
+            d2[unit] = work.tile([P, PACK, n // PACK], F32, tag="d2", name="d2")
+            nc.vector.scalar_tensor_tensor(
+                out=d2[unit][:],
+                in0=acc[unit][:].rearrange("p (q t) -> p t q", t=PACK),
+                scalar=-2.0,
+                in1=place(s_all[:, n0 // BLOCK], unit),
+                op0=ALU.mult,
+                op1=ALU.add,
+            )
+            nc.vector.tensor_scalar(
+                out=d2[unit][:], in0=d2[unit][:],
+                scalar1=c_col[:, jt : jt + 1], scalar2=0.0, op0=ALU.add, op1=ALU.max,
+            )
+
+        def root(unit):
+            nc.scalar.activation(out=d2[unit][:], in_=d2[unit][:], func=ACT.Sqrt)
+
+        def exponential(unit):
+            jt, n0, n = unit
+            column = n0 // BLOCK if n0 + n < NTR else BLOCKS
+            nc.scalar.activation(
+                out=place(kern[:, jt, n0 // BLOCK], unit), in_=d2[unit][:], func=ACT.Exp,
+                scale=-1.0 / GAMMA, accum_out=ksum[:, jt, column : column + 1],
+            )
+
+        def open_banks(pool, tag, units):
+            for unit in units:
+                acc[unit] = pool.tile([P, unit[2]], F32, tag=tag, name="acc_%d_%d" % unit[:2])
+
+        def narrow_load(first, passes, n0, n):
+            sm = narrow.tile([P, passes, n], I32, align_bytes=64, tag="sm", name="sm")
+            nc.sync.dma_start(
+                out=sm[:],
+                in_=sM_words[first : first + passes, :, n0 : n0 + n, :]
+                .rearrange("g p n t -> p g (n t)")
+                .bitcast(I32),
+            )
+            return sm
+
+        issue(LOOKAHEAD)
+        reorder(0)
+        prepare(0)
         for blk in range(BLOCKS):
-            s_bank = psum.tile([P, BLOCK], F32, tag="bank")
+            s_bank = psum_wide.tile([P, BLOCK], F32, tag="wide", name="s_bank")
             nc.tensor.matmul(
                 out=s_bank[:], lhsT=ones[:], rhs=s_row[:, blk * BLOCK : (blk + 1) * BLOCK],
                 start=True, stop=True,
             )
-            nc.vector.tensor_copy(
-                out=s_all[:, blk], in_=s_bank[:].rearrange("p (q t) -> p t q", t=PACK)
-            )
+            nc.scalar.copy(out=s_all[:, blk], in_=s_bank[:].rearrange("p (q t) -> p t q", t=PACK))
+        nc.vector.tensor_copy(out=c_col[:], in_=c_bf16[:])
 
-        kern = keep.tile([P, TEST_TILES, BLOCKS, PACK, P], F32)
-        ksum = keep.tile([P, TEST_TILES, BLOCKS], F32)
-        for blocks in ROUND_BLOCKS:
-            units = [(jt, blk) for jt in range(TEST_TILES) for blk in blocks]
-            first_col = blocks[0] * BLOCK
-            width = len(blocks) * BLOCK
-            chunk = STREAM_WORDS // width
-            acc = {}
-            for jt, blk in units:
-                acc[jt, blk] = psum.tile([P, BLOCK], F32, tag="bank", name="acc_%d_%d" % (jt, blk))
-            for first in range(0, FEAT_PASSES, chunk):
-                sm = stream.tile([P, chunk, width], I32, align_bytes=64, tag="sm")
-                nc.sync.dma_start(
-                    out=sm[:],
-                    in_=sM_words[first : first + chunk, :, first_col : first_col + width, :]
-                    .rearrange("g p n t -> p g (n t)")
-                    .bitcast(I32),
-                )
-                for i in range(chunk):
-                    g = first + i
-                    a, b = divmod(g, GROUP)
-                    for jt, blk in units:
-                        local = (blk - blocks[0]) * BLOCK
-                        nc.tensor.matmul_mx(
-                            out=acc[jt, blk][:],
-                            lhsT=x_codes[:, g, jt * P : (jt + 1) * P].bitcast(FP8X4),
-                            lhsT_scale=x_planes[:, g, jt * P : (jt + 1) * P],
-                            rhs=sm[:, i, local : local + BLOCK].bitcast(FP8X4),
-                            rhs_scale=sm_planes[b * SCALE_ROWS : P, a, blk * BLOCK : (blk + 1) * BLOCK],
-                            start=(g == 0),
-                            stop=(g == FEAT_PASSES - 1),
-                        )
-            d2, clamped, dist = {}, {}, {}
-            for jt, blk in units:
-                d2[jt, blk] = work.tile([P, PACK, P], F32, tag="d2", name="d2_%d_%d" % (jt, blk))
-                nc.vector.scalar_tensor_tensor(
-                    out=d2[jt, blk][:],
-                    in0=acc[jt, blk][:].rearrange("p (q t) -> p t q", t=PACK),
-                    scalar=-2.0,
-                    in1=s_all[:, blk],
-                    op0=ALU.mult,
-                    op1=ALU.add,
-                )
-            for jt, blk in units:
-                clamped[jt, blk] = work.tile(
-                    [P, PACK, P], F32, tag="clamped", name="clamped_%d_%d" % (jt, blk)
-                )
-                nc.vector.tensor_scalar(
-                    out=clamped[jt, blk][:], in0=d2[jt, blk][:],
-                    scalar1=c_col[:, jt : jt + 1], scalar2=0.0, op0=ALU.add, op1=ALU.max,
-                )
-            for jt, blk in units:
-                dist[jt, blk] = work.tile([P, PACK, P], F32, tag="dist", name="dist_%d_%d" % (jt, blk))
-                nc.scalar.activation(out=dist[jt, blk][:], in_=clamped[jt, blk][:], func=ACT.Sqrt)
-            for jt, blk in units:
-                nc.scalar.activation(
-                    out=kern[:, jt, blk], in_=dist[jt, blk][:], func=ACT.Exp, scale=-1.0 / GAMMA,
-                    accum_out=ksum[:, jt, blk : blk + 1],
-                )
+        first_units = [(jt, blk * BLOCK, BLOCK) for jt in range(TEST_TILES) for blk in range(WIDE)]
+        open_banks(psum_wide, "wide", first_units)
+        for g in range(FEAT_PASSES):
+            issue(g + LOOKAHEAD)
+            if g == 1 or (g % STEP == 0 and 0 < g < FEAT_PASSES - STEP):
+                prepare((g + STEP) // STEP if g > 1 else 1)
+            for unit in first_units:
+                multiply(g, sm_tiles[g][:, unit[1] : unit[1] + BLOCK], unit)
 
-        for quad in QUAD_ORDER:
-            nc.sync.dma_start(
-                out=y_planes[quad * QUADRANT : quad * QUADRANT + live, :].bitcast(I32),
-                in_=y_train_scales[:, quad * SCALE_ROWS : (quad + 1) * SCALE_ROWS, :].bitcast(I32),
-            )
+        n0 = WIDE * BLOCK
+        second_units = [(jt, n0, BLOCK) for jt in range(TEST_TILES)]
+        tiles = [narrow_load(first, STEP, n0, BLOCK) for first in range(0, FEAT_PASSES, STEP)]
+        open_banks(psum_turn, "turn", second_units)
+        for first in range(0, FEAT_PASSES, STEP):
+            for unit in second_units:
+                for i in range(STEP):
+                    multiply(first + i, tiles[first // STEP][:, i, :], unit)
+        for unit in first_units:
+            squared_distance(unit)
+        for unit in first_units:
+            root(unit)
+        for unit in first_units:
+            exponential(unit)
+
+        n0 = (BLOCKS - 1) * BLOCK
+        left_units = [(jt, n0, HALF) for jt in range(TEST_TILES)]
+        right_units = [(jt, n0 + HALF, HALF) for jt in range(TEST_TILES)]
+        tiles = [narrow_load(first, STEP, n0, BLOCK) for first in range(0, SPLIT, STEP)]
+        left = narrow_load(SPLIT, FEAT_PASSES - SPLIT, n0, HALF)
+        right = narrow_load(SPLIT, FEAT_PASSES - SPLIT, n0 + HALF, HALF)
+        load_scales(nc.sync, I32, y_planes, y_train_scales)
         y_codes = keep.tile([P, BLOCKS, C], I32, align_bytes=64)
         nc.sync.dma_start(
             out=y_codes[:], in_=y_train_words.rearrange("g p n t -> p g (n t)").bitcast(I32)
         )
+        open_banks(psum_turn, "turn", left_units)
+        open_banks(psum_wide, "wide", right_units)
+        for g in range(SPLIT):
+            for jt in range(TEST_TILES):
+                multiply(g, tiles[g // STEP][:, g % STEP, :HALF], left_units[jt])
+                multiply(g, tiles[g // STEP][:, g % STEP, HALF:], right_units[jt])
+        for unit in second_units:
+            squared_distance(unit)
+        spare = keep.tile([P, 1], F32)
+        for unit in second_units:
+            root(unit)
+        for unit in second_units:
+            exponential(unit)
+        nc.scalar.activation(out=spare[:], in_=ksum[:, 0, 0:1], func=ACT.Sqrt)
+        for words, units in ((left, left_units), (right, right_units)):
+            for unit in units:
+                for g in range(SPLIT, FEAT_PASSES):
+                    multiply(g, words[:, g - SPLIT, :], unit)
+            for unit in units:
+                squared_distance(unit)
+            for unit in units:
+                root(unit)
+        for jt in range(TEST_TILES):
+            exponential(left_units[jt])
+            exponential(right_units[jt])
+        warm = psum_turn.tile([P, BLOCK], F32, tag="turn", name="warm")
+        for i in range(WARM):
+            nc.tensor.matmul(out=warm[:], lhsT=ones[:], rhs=s_row[:, :BLOCK], start=True, stop=True)
 
         total = keep.tile([P, TEST_TILES], F32)
         rsum = keep.tile([P, TEST_TILES], F32)
         w_codes = keep.tile([P, TEST_TILES, BLOCKS, P], U32, align_bytes=64)
         w_planes = keep.tile([P, TEST_TILES, BLOCKS, P], U8, align_bytes=64)
-        for jt in range(TEST_TILES):
+        pieces = [(jt, blk) for jt in range(TEST_TILES) for blk in range(BLOCKS)]
+        on_scalar = [(1, 0), (1, 1)]
+        w_bf16, w_grouped, o_bank = {}, {}, {}
+
+        def reciprocal_sum(jt):
             nc.vector.tensor_reduce(
                 out=total[:, jt : jt + 1], in_=ksum[:, jt, :], axis=AXIS.X, op=ALU.add
             )
             nc.vector.reciprocal(out=rsum[:, jt : jt + 1], in_=total[:, jt : jt + 1])
-            for blk in range(BLOCKS):
-                w_bf16 = work.tile([P, PACK, P], BF16)
+
+        def normalise(piece):
+            jt, blk = piece
+            w_bf16[piece] = work.tile([P, PACK, P], BF16, tag="w_bf16", name="w_bf16")
+            if piece in on_scalar:
+                nc.scalar.activation(
+                    out=w_bf16[piece][:], in_=kern[:, jt, blk], func=ACT.Copy, scale=rsum[:, jt : jt + 1]
+                )
+            else:
                 nc.vector.tensor_scalar(
-                    out=w_bf16[:], in0=kern[:, jt, blk], scalar1=rsum[:, jt : jt + 1], scalar2=None,
-                    op0=ALU.mult,
+                    out=w_bf16[piece][:], in0=kern[:, jt, blk], scalar1=rsum[:, jt : jt + 1],
+                    scalar2=None, op0=ALU.mult,
                 )
-                wt = psum.tile([P, PACK, P], BF16, tag="bank")
-                for t in range(PACK):
-                    nc.tensor.transpose(wt[:, t, :], w_bf16[:, t, :], ident_bf16[:])
-                w_grouped = work.tile([P, P, PACK], BF16, align_bytes=64)
-                nc.scalar.copy(out=w_grouped[:], in_=wt[:].rearrange("p t j -> p j t"))
-                nc.vector.quantize_mx(
-                    out=w_codes[:, jt, blk, :].bitcast(FP8X4),
-                    scales=w_planes[:, jt, blk, :],
-                    in_=w_grouped[:].rearrange("p j t -> p (j t)"),
-                )
-        for jt in range(TEST_TILES):
-            o_bank = psum.tile([P, C], F32, tag="bank")
-            for blk in range(BLOCKS):
-                nc.tensor.matmul_mx(
-                    out=o_bank[:],
-                    lhsT=w_codes[:, jt, blk, :].bitcast(FP8X4),
-                    lhsT_scale=w_planes[:, jt, blk, :],
-                    rhs=y_codes[:, blk, :].bitcast(FP8X4),
-                    rhs_scale=y_planes[blk * SCALE_ROWS : P, :],
-                    start=(blk == 0),
-                    stop=(blk == BLOCKS - 1),
-                )
-            result = work.tile([P, C], F32)
-            nc.vector.tensor_copy(out=result[:], in_=o_bank[:])
-            nc.sync.dma_start(out=out[jt * P : (jt + 1) * P, :], in_=result[:])
+
+        def turn(piece):
+            if piece == pieces[1]:
+                for other in on_scalar:
+                    normalise(other)
+            wt = psum_wide.tile([P, PACK, P], BF16, tag="wide", name="wt")
+            for t in range(PACK):
+                nc.tensor.transpose(wt[:, t, :], w_bf16[piece][:, t, :], ident_bf16[:])
+            w_grouped[piece] = work.tile([P, P, PACK], BF16, align_bytes=64, tag="w_grouped", name="w_grouped")
+            nc.scalar.copy(out=w_grouped[piece][:], in_=wt[:].rearrange("p t j -> p j t"))
+
+        def quantise(piece):
+            jt, blk = piece
+            nc.vector.quantize_mx(
+                out=w_codes[:, jt, blk, :].bitcast(FP8X4),
+                scales=w_planes[:, jt, blk, :],
+                in_=w_grouped[piece][:].rearrange("p j t -> p (j t)"),
+            )
+
+        def second_product(piece):
+            jt, blk = piece
+            if blk == 0:
+                o_bank[jt] = psum_turn.tile([P, C], F32, tag="turn", name="o_bank")
+            nc.tensor.matmul_mx(
+                out=o_bank[jt][:],
+                lhsT=w_codes[:, jt, blk, :].bitcast(FP8X4),
+                lhsT_scale=w_planes[:, jt, blk, :],
+                rhs=y_codes[:, blk, :].bitcast(FP8X4),
+                rhs_scale=y_planes[blk * SCALE_ROWS : P, :],
+                start=(blk == 0),
+                stop=(blk == BLOCKS - 1),
+            )
+            if blk == BLOCKS - 1:
+                result = work.tile([P, C], F32, name="result")
+                nc.vector.tensor_copy(out=result[:], in_=o_bank[jt][:])
+                nc.sync.dma_start(out=out[jt * P : (jt + 1) * P, :], in_=result[:])
+
+        reciprocal_sum(0)
+        lag, depth = 3, 5
+        for n in range(len(pieces) + depth):
+            if n == 1:
+                reciprocal_sum(1)
+            if n < len(pieces):
+                if pieces[n] not in on_scalar:
+                    normalise(pieces[n])
+                turn(pieces[n])
+            if lag <= n < len(pieces) + lag:
+                quantise(pieces[n - lag])
+            if n >= depth:
+                second_product(pieces[n - depth])

@@ -60,11 +60,11 @@ def tile_rbfnet_pb_k_kernel(
             sm_planes.append(plane)
         y_planes = keep.tile([P, C], U8, align_bytes=64)
 
-        def load_scales(queue, dtype, plane, source):
+        def load_scales(plane, source):
             for quad in QUAD_ORDER:
-                queue.dma_start(
-                    out=plane[quad * QUADRANT : quad * QUADRANT + LIVE, :].bitcast(dtype),
-                    in_=source[:, quad * SCALE_ROWS : (quad + 1) * SCALE_ROWS, :].bitcast(dtype),
+                nc.sync.dma_start(
+                    out=plane[quad * QUADRANT : quad * QUADRANT + LIVE, :].bitcast(I32),
+                    in_=source[:, quad * SCALE_ROWS : (quad + 1) * SCALE_ROWS, :].bitcast(I32),
                 )
 
         nc.vector.memset(sm_planes[0][:].bitcast(I32), 0)
@@ -79,8 +79,7 @@ def tile_rbfnet_pb_k_kernel(
         ones = keep.tile([P, P], BF16)
         nc.vector.memset(ones[:], 1.0)
         for a in range(1, GROUPS):
-            nc.gpsimd.memset(sm_planes[a][:].bitcast(I32), 0)
-            load_scales(nc.gpsimd, F32, sm_planes[a], sM_scales[a * GROUP : (a + 1) * GROUP])
+            nc.vector.memset(sm_planes[a][:].bitcast(I32), 0)
         nc.gpsimd.memset(y_planes[:].bitcast(I32), 0)
         ident_bf16 = keep.tile([P, P], BF16)
         make_identity(nc, ident_bf16[:])
@@ -97,7 +96,8 @@ def tile_rbfnet_pb_k_kernel(
                 kind, first, count = order[0]
                 order.remove(order[0])
                 if kind == "s":
-                    load_scales(nc.sync, I32, sm_planes[0], sM_scales[:GROUP])
+                    for a in range(GROUPS):
+                        load_scales(sm_planes[a], sM_scales[a * GROUP : (a + 1) * GROUP])
                 elif kind == "x":
                     cols = slice(first * K_PASS, (first + count) * K_PASS)
                     for jt in range(TEST_TILES):
@@ -257,7 +257,7 @@ def tile_rbfnet_pb_k_kernel(
         tiles = [narrow_load(first, STEP, n0, BLOCK) for first in range(0, SPLIT, STEP)]
         left = narrow_load(SPLIT, FEAT_PASSES - SPLIT, n0, HALF)
         right = narrow_load(SPLIT, FEAT_PASSES - SPLIT, n0 + HALF, HALF)
-        load_scales(nc.sync, I32, y_planes, y_train_scales)
+        load_scales(y_planes, y_train_scales)
         y_codes = keep.tile([P, BLOCKS, C], I32, align_bytes=64)
         nc.sync.dma_start(
             out=y_codes[:], in_=y_train_words.rearrange("g p n t -> p g (n t)").bitcast(I32)

@@ -32,8 +32,7 @@ LIVE = GROUP * SCALE_ROWS
 QUAD_ORDER = (0, 2, 1, 3)
 WIDE = 2
 STEP = 2
-STEPS = FEAT_PASSES // STEP
-SPLIT = 12
+SPLIT = 8
 LOOKAHEAD = 6
 WARM = 16
 
@@ -46,9 +45,9 @@ def tile_rbfnet_pb_k_kernel(
     nc = tc.nc
     with ExitStack() as stack:
         keep = stack.enter_context(tc.tile_pool(name="keep", bufs=1))
-        xstage = stack.enter_context(tc.tile_pool(name="xstage", bufs=3))
+        xstage = stack.enter_context(tc.tile_pool(name="xstage", bufs=2))
         stream = stack.enter_context(tc.tile_pool(name="stream", bufs=LOOKAHEAD + 2))
-        narrow = stack.enter_context(tc.tile_pool(name="narrow", bufs=14))
+        narrow = stack.enter_context(tc.tile_pool(name="narrow", bufs=10))
         work = stack.enter_context(tc.tile_pool(name="work", bufs=4))
         psum_wide = stack.enter_context(tc.psum_pool(name="psum_wide", bufs=4))
         psum_turn = stack.enter_context(tc.psum_pool(name="psum_turn", bufs=4))
@@ -56,9 +55,9 @@ def tile_rbfnet_pb_k_kernel(
 
         sm_planes = []
         for a in range(GROUPS):
-            plane = keep.tile([P, NTR], U8, align_bytes=64, name="sm_planes_%d" % a)
+            plane = keep.tile([P, NTR], U8, align_bytes=256, name="sm_planes_%d" % a)
             sm_planes.append(plane)
-        y_planes = keep.tile([P, C], U8, align_bytes=64)
+        y_planes = keep.tile([P, C], U8, align_bytes=256)
 
         def load_scales(plane, source):
             for quad in QUAD_ORDER:
@@ -87,17 +86,17 @@ def tile_rbfnet_pb_k_kernel(
         x_raw = keep.tile([P, TEST_TILES, D], BF16)
         sm_tiles = {}
         order = [("x", 0, 2), ("s", 0, 0), ("m", 0, 1), ("x", 2, 2), ("m", 1, 1), ("x", 4, 4)]
-        order += [("m", g, 1) for g in range(2, 6)] + [("x", 8, 4)]
-        order += [("m", g, 1) for g in range(6, 10)] + [("x", 12, 4)]
-        order += [("m", g, 1) for g in range(10, FEAT_PASSES)]
+        order += [("m", g, 1) for g in range(2, 4)] + [("s", 1, 0), ("x", 8, 4)]
+        order += [("m", g, 1) for g in range(4, 8)] + [("s", 2, 0), ("x", 12, 4)]
+        order += [("m", g, 1) for g in range(8, 12)] + [("s", 3, 0)]
+        order += [("m", g, 1) for g in range(12, FEAT_PASSES)]
 
         def issue(last_pass):
             while order and (order[0][0] != "m" or order[0][1] <= last_pass):
                 kind, first, count = order[0]
                 order.remove(order[0])
                 if kind == "s":
-                    for a in range(GROUPS):
-                        load_scales(sm_planes[a], sM_scales[a * GROUP : (a + 1) * GROUP])
+                    load_scales(sm_planes[first], sM_scales[first * GROUP : (first + 1) * GROUP])
                 elif kind == "x":
                     cols = slice(first * K_PASS, (first + count) * K_PASS)
                     for jt in range(TEST_TILES):
@@ -106,7 +105,7 @@ def tile_rbfnet_pb_k_kernel(
                         )
                 else:
                     sm_tiles[first] = stream.tile(
-                        [P, WIDE * BLOCK], I32, align_bytes=64, tag="sm", name="sm_%d" % first
+                        [P, WIDE * BLOCK], I32, align_bytes=256, tag="sm", name="sm_%d" % first
                     )
                     nc.sync.dma_start(
                         out=sm_tiles[first][:],
@@ -116,42 +115,38 @@ def tile_rbfnet_pb_k_kernel(
                     )
 
         x_words = x_raw[:].bitcast(F32)
-        x_codes = keep.tile([P, FEAT_PASSES, NTE], U32, align_bytes=64)
-        x_planes = keep.tile([P, FEAT_PASSES, NTE], U8, align_bytes=64)
+        x_codes = keep.tile([P, FEAT_PASSES, NTE], U32, align_bytes=256)
+        x_planes = keep.tile([P, FEAT_PASSES, NTE], U8, align_bytes=256)
         half = K_PASS // 2
-        runs = {}
 
-        def reorder(step):
-            runs[step] = xstage.tile([P, TEST_TILES, STEP, 2, P], F32, tag="runs", name="runs")
+        def prepare(first, count):
+            runs = xstage.tile([P, TEST_TILES, count, 2, P], F32, tag="runs", name="runs")
             for jt in range(TEST_TILES):
                 nc.vector.tensor_copy(
-                    out=runs[step][:, jt],
-                    in_=x_words[:, jt, step * STEP * half : (step + 1) * STEP * half].rearrange(
-                        "j (g p u) -> j g u p", g=STEP, u=2
+                    out=runs[:, jt],
+                    in_=x_words[:, jt, first * half : (first + count) * half].rearrange(
+                        "j (g p u) -> j g u p", g=count, u=2
                     ),
                 )
-
-        def prepare(step):
-            grouped = xstage.tile([P, STEP, TEST_TILES, P, PACK], BF16, align_bytes=64, name="grouped")
+            grouped = xstage.tile([P, count, TEST_TILES, P, PACK], BF16, align_bytes=256, tag="grouped", name="grouped")
             grouped_words = grouped[:].bitcast(F32)
-            for i in range(STEP):
+            for i in range(count):
                 xt = psum_turn.tile([P, TEST_TILES, 2, P], F32, tag="turn", name="xt")
                 for jt in range(TEST_TILES):
                     for u in range(2):
-                        nc.tensor.transpose(xt[:, jt, u, :], runs[step][:, jt, i, u, :], ident_f32[:])
-                copy = nc.vector.tensor_copy if i == STEP - 1 else nc.scalar.copy
+                        nc.tensor.transpose(xt[:, jt, u, :], runs[:, jt, i, u, :], ident_f32[:])
+                copy = nc.vector.tensor_copy if i % 2 else nc.scalar.copy
                 copy(out=grouped_words[:, i], in_=xt[:].rearrange("p a u j -> p a j u"))
-            passes = slice(step * STEP, (step + 1) * STEP)
+            passes = slice(first, first + count)
             nc.vector.quantize_mx(
                 out=x_codes[:, passes, :].rearrange("p g j -> p (g j)").bitcast(FP8X4),
                 scales=x_planes[:, passes, :].rearrange("p g j -> p (g j)"),
                 in_=grouped[:].rearrange("p g a j t -> p (g a j t)"),
             )
-            if step + 1 < STEPS:
-                reorder(step + 1)
 
         kern = keep.tile([P, TEST_TILES, BLOCKS, PACK, P], F32)
-        ksum = keep.tile([P, TEST_TILES, BLOCKS + 1], F32)
+        ksum = keep.tile([P, TEST_TILES, BLOCKS], F32)
+        last_d2 = keep.tile([P, TEST_TILES, PACK, P], F32)
         s_all = keep.tile([P, BLOCKS, PACK, P], BF16)
         c_col = keep.tile([P, TEST_TILES], F32)
         acc, d2 = {}, {}
@@ -176,9 +171,13 @@ def tile_rbfnet_pb_k_kernel(
 
         def squared_distance(unit):
             jt, n0, n = unit
-            d2[unit] = work.tile([P, PACK, n // PACK], F32, tag="d2", name="d2")
+            if n == BLOCK:
+                whole = work.tile([P, PACK, P], F32, tag="d2", name="d2")
+                d2[unit] = whole[:]
+            else:
+                d2[unit] = place(last_d2[:, jt], unit)
             nc.vector.scalar_tensor_tensor(
-                out=d2[unit][:],
+                out=d2[unit],
                 in0=acc[unit][:].rearrange("p (q t) -> p t q", t=PACK),
                 scalar=-2.0,
                 in1=place(s_all[:, n0 // BLOCK], unit),
@@ -186,27 +185,25 @@ def tile_rbfnet_pb_k_kernel(
                 op1=ALU.add,
             )
             nc.vector.tensor_scalar(
-                out=d2[unit][:], in0=d2[unit][:],
+                out=d2[unit], in0=d2[unit],
                 scalar1=c_col[:, jt : jt + 1], scalar2=0.0, op0=ALU.add, op1=ALU.max,
             )
 
         def root(unit):
-            nc.scalar.activation(out=d2[unit][:], in_=d2[unit][:], func=ACT.Sqrt)
+            nc.scalar.activation(out=d2[unit], in_=d2[unit], func=ACT.Sqrt)
 
-        def exponential(unit):
-            jt, n0, n = unit
-            column = n0 // BLOCK if n0 + n < NTR else BLOCKS
+        def exponential(jt, blk, source):
             nc.scalar.activation(
-                out=place(kern[:, jt, n0 // BLOCK], unit), in_=d2[unit][:], func=ACT.Exp,
-                scale=-1.0 / GAMMA, accum_out=ksum[:, jt, column : column + 1],
+                out=kern[:, jt, blk], in_=source, func=ACT.Exp,
+                scale=-1.0 / GAMMA, accum_out=ksum[:, jt, blk : blk + 1],
             )
 
         def open_banks(pool, tag, units):
             for unit in units:
                 acc[unit] = pool.tile([P, unit[2]], F32, tag=tag, name="acc_%d_%d" % unit[:2])
 
-        def narrow_load(first, passes, n0, n):
-            sm = narrow.tile([P, passes, n], I32, align_bytes=64, tag="sm", name="sm")
+        def narrow_load(pool, tag, first, passes, n0, n):
+            sm = pool.tile([P, passes, n], I32, align_bytes=256, tag=tag, name="sm")
             nc.sync.dma_start(
                 out=sm[:],
                 in_=sM_words[first : first + passes, :, n0 : n0 + n, :]
@@ -216,8 +213,7 @@ def tile_rbfnet_pb_k_kernel(
             return sm
 
         issue(LOOKAHEAD)
-        reorder(0)
-        prepare(0)
+        prepare(0, 2)
         for blk in range(BLOCKS):
             s_bank = psum_wide.tile([P, BLOCK], F32, tag="wide", name="s_bank")
             nc.tensor.matmul(
@@ -229,16 +225,17 @@ def tile_rbfnet_pb_k_kernel(
 
         first_units = [(jt, blk * BLOCK, BLOCK) for jt in range(TEST_TILES) for blk in range(WIDE)]
         open_banks(psum_wide, "wide", first_units)
+        ahead = {1: (2, 2), 2: (4, 4), 4: (8, 4), 8: (12, 4)}
         for g in range(FEAT_PASSES):
             issue(g + LOOKAHEAD)
-            if g == 1 or (g % STEP == 0 and 0 < g < FEAT_PASSES - STEP):
-                prepare((g + STEP) // STEP if g > 1 else 1)
+            if g in ahead:
+                prepare(*ahead[g])
             for unit in first_units:
                 multiply(g, sm_tiles[g][:, unit[1] : unit[1] + BLOCK], unit)
 
         n0 = WIDE * BLOCK
         second_units = [(jt, n0, BLOCK) for jt in range(TEST_TILES)]
-        tiles = [narrow_load(first, STEP, n0, BLOCK) for first in range(0, FEAT_PASSES, STEP)]
+        tiles = [narrow_load(narrow, "sm", first, STEP, n0, BLOCK) for first in range(0, FEAT_PASSES, STEP)]
         open_banks(psum_turn, "turn", second_units)
         for first in range(0, FEAT_PASSES, STEP):
             for unit in second_units:
@@ -249,16 +246,16 @@ def tile_rbfnet_pb_k_kernel(
         for unit in first_units:
             root(unit)
         for unit in first_units:
-            exponential(unit)
+            exponential(unit[0], unit[1] // BLOCK, d2[unit])
 
         n0 = (BLOCKS - 1) * BLOCK
         left_units = [(jt, n0, HALF) for jt in range(TEST_TILES)]
         right_units = [(jt, n0 + HALF, HALF) for jt in range(TEST_TILES)]
-        tiles = [narrow_load(first, STEP, n0, BLOCK) for first in range(0, SPLIT, STEP)]
-        left = narrow_load(SPLIT, FEAT_PASSES - SPLIT, n0, HALF)
-        right = narrow_load(SPLIT, FEAT_PASSES - SPLIT, n0 + HALF, HALF)
+        tiles = [narrow_load(narrow, "sm", first, STEP, n0, BLOCK) for first in range(0, SPLIT, STEP)]
+        left = narrow_load(keep, "left", SPLIT, FEAT_PASSES - SPLIT, n0, HALF)
+        right = narrow_load(keep, "right", SPLIT, FEAT_PASSES - SPLIT, n0 + HALF, HALF)
         load_scales(y_planes, y_train_scales)
-        y_codes = keep.tile([P, BLOCKS, C], I32, align_bytes=64)
+        y_codes = keep.tile([P, BLOCKS, C], I32, align_bytes=256)
         nc.sync.dma_start(
             out=y_codes[:], in_=y_train_words.rearrange("g p n t -> p g (n t)").bitcast(I32)
         )
@@ -274,7 +271,7 @@ def tile_rbfnet_pb_k_kernel(
         for unit in second_units:
             root(unit)
         for unit in second_units:
-            exponential(unit)
+            exponential(unit[0], unit[1] // BLOCK, d2[unit])
         nc.scalar.activation(out=spare[:], in_=ksum[:, 0, 0:1], func=ACT.Sqrt)
         for words, units in ((left, left_units), (right, right_units)):
             for unit in units:
@@ -285,16 +282,15 @@ def tile_rbfnet_pb_k_kernel(
             for unit in units:
                 root(unit)
         for jt in range(TEST_TILES):
-            exponential(left_units[jt])
-            exponential(right_units[jt])
+            exponential(jt, BLOCKS - 1, last_d2[:, jt])
         warm = psum_turn.tile([P, BLOCK], F32, tag="turn", name="warm")
         for i in range(WARM):
             nc.tensor.matmul(out=warm[:], lhsT=ones[:], rhs=s_row[:, :BLOCK], start=True, stop=True)
 
         total = keep.tile([P, TEST_TILES], F32)
         rsum = keep.tile([P, TEST_TILES], F32)
-        w_codes = keep.tile([P, TEST_TILES, BLOCKS, P], U32, align_bytes=64)
-        w_planes = keep.tile([P, TEST_TILES, BLOCKS, P], U8, align_bytes=64)
+        w_codes = keep.tile([P, TEST_TILES, BLOCKS, P], U32, align_bytes=256)
+        w_planes = keep.tile([P, TEST_TILES, BLOCKS, P], U8, align_bytes=256)
         pieces = [(jt, blk) for jt in range(TEST_TILES) for blk in range(BLOCKS)]
         on_scalar = [(1, 0), (1, 1)]
         w_bf16, w_grouped, o_bank = {}, {}, {}
@@ -325,7 +321,7 @@ def tile_rbfnet_pb_k_kernel(
             wt = psum_wide.tile([P, PACK, P], BF16, tag="wide", name="wt")
             for t in range(PACK):
                 nc.tensor.transpose(wt[:, t, :], w_bf16[piece][:, t, :], ident_bf16[:])
-            w_grouped[piece] = work.tile([P, P, PACK], BF16, align_bytes=64, tag="w_grouped", name="w_grouped")
+            w_grouped[piece] = work.tile([P, P, PACK], BF16, align_bytes=256, tag="w_grouped", name="w_grouped")
             nc.scalar.copy(out=w_grouped[piece][:], in_=wt[:].rearrange("p t j -> p j t"))
 
         def quantise(piece):

@@ -33,7 +33,7 @@ QUAD_ORDER = (0, 2, 1, 3)
 WIDE = 2
 STEP = 2
 SPLIT = 8
-LOOKAHEAD = 6
+LOOKAHEAD = 10
 WARM = 16
 
 FLOPS = 2 * NTR * D * NTE + 2 * NTE * NTR * C
@@ -59,45 +59,42 @@ def tile_rbfnet_pb_k_kernel(
             sm_planes.append(plane)
         y_planes = keep.tile([P, C], U8, align_bytes=256)
 
-        def load_scales(plane, source):
+        def load_scales(queue, dtype, plane, source):
             for quad in QUAD_ORDER:
-                nc.sync.dma_start(
-                    out=plane[quad * QUADRANT : quad * QUADRANT + LIVE, :].bitcast(I32),
-                    in_=source[:, quad * SCALE_ROWS : (quad + 1) * SCALE_ROWS, :].bitcast(I32),
+                queue.dma_start(
+                    out=plane[quad * QUADRANT : quad * QUADRANT + LIVE, :].bitcast(dtype),
+                    in_=source[:, quad * SCALE_ROWS : (quad + 1) * SCALE_ROWS, :].bitcast(dtype),
                 )
 
-        nc.vector.memset(sm_planes[0][:].bitcast(I32), 0)
+        ident_f32 = keep.tile([P, P], F32)
+        make_identity(nc, ident_f32[:])
         s_row = keep.tile([P, NTR], BF16)
-        nc.gpsimd.memset(s_row[:].bitcast(I32), 0)
+        nc.vector.memset(sm_planes[0][:].bitcast(I32), 0)
+        nc.vector.memset(s_row[:].bitcast(I32), 0)
+        for a in range(GROUPS):
+            if a > 0:
+                nc.vector.memset(sm_planes[a][:].bitcast(I32), 0)
+            load_scales(nc.gpsimd, F32, sm_planes[a], sM_scales[a * GROUP : (a + 1) * GROUP])
         nc.scalar.dma_start(out=s_row[0:1, :], in_=s_norm2.rearrange("(o n) -> o n", o=1))
         c_bf16 = keep.tile([P, TEST_TILES], BF16)
         with nc.allow_non_contiguous_dma(reason="256 two-byte values, one to a partition"):
             nc.scalar.dma_start(out=c_bf16[:], in_=c_norm2.rearrange("(a p) -> p a", p=P))
-        ident_f32 = keep.tile([P, P], F32)
-        make_identity(nc, ident_f32[:])
         ones = keep.tile([P, P], BF16)
         nc.vector.memset(ones[:], 1.0)
-        for a in range(1, GROUPS):
-            nc.vector.memset(sm_planes[a][:].bitcast(I32), 0)
         nc.gpsimd.memset(y_planes[:].bitcast(I32), 0)
         ident_bf16 = keep.tile([P, P], BF16)
         make_identity(nc, ident_bf16[:])
 
         x_raw = keep.tile([P, TEST_TILES, D], BF16)
         sm_tiles = {}
-        order = [("x", 0, 2), ("s", 0, 0), ("m", 0, 1), ("x", 2, 2), ("m", 1, 1), ("x", 4, 4)]
-        order += [("m", g, 1) for g in range(2, 4)] + [("s", 1, 0), ("x", 8, 4)]
-        order += [("m", g, 1) for g in range(4, 8)] + [("s", 2, 0), ("x", 12, 4)]
-        order += [("m", g, 1) for g in range(8, 12)] + [("s", 3, 0)]
-        order += [("m", g, 1) for g in range(12, FEAT_PASSES)]
+        order = [("x", 0, 4), ("x", 4, 4), ("x", 8, 8)]
+        order += [("m", g, 1) for g in range(FEAT_PASSES)]
 
         def issue(last_pass):
             while order and (order[0][0] != "m" or order[0][1] <= last_pass):
                 kind, first, count = order[0]
                 order.remove(order[0])
-                if kind == "s":
-                    load_scales(sm_planes[first], sM_scales[first * GROUP : (first + 1) * GROUP])
-                elif kind == "x":
+                if kind == "x":
                     cols = slice(first * K_PASS, (first + count) * K_PASS)
                     for jt in range(TEST_TILES):
                         nc.sync.dma_start(
@@ -120,22 +117,17 @@ def tile_rbfnet_pb_k_kernel(
         half = K_PASS // 2
 
         def prepare(first, count):
-            runs = xstage.tile([P, TEST_TILES, count, 2, P], F32, tag="runs", name="runs")
-            for jt in range(TEST_TILES):
-                nc.vector.tensor_copy(
-                    out=runs[:, jt],
-                    in_=x_words[:, jt, first * half : (first + count) * half].rearrange(
-                        "j (g p u) -> j g u p", g=count, u=2
-                    ),
-                )
             grouped = xstage.tile([P, count, TEST_TILES, P, PACK], BF16, align_bytes=256, tag="grouped", name="grouped")
             grouped_words = grouped[:].bitcast(F32)
             for i in range(count):
                 xt = psum_turn.tile([P, TEST_TILES, 2, P], F32, tag="turn", name="xt")
                 for jt in range(TEST_TILES):
                     for u in range(2):
-                        nc.tensor.transpose(xt[:, jt, u, :], runs[:, jt, i, u, :], ident_f32[:])
-                copy = nc.vector.tensor_copy if i % 2 else nc.scalar.copy
+                        word = (first + i) * half + u
+                        nc.tensor.transpose(
+                            xt[:, jt, u, :], x_words[:, jt, word : word + half - u : 2], ident_f32[:]
+                        )
+                copy = nc.vector.tensor_copy if i % 4 == 3 else nc.scalar.copy
                 copy(out=grouped_words[:, i], in_=xt[:].rearrange("p a u j -> p a j u"))
             passes = slice(first, first + count)
             nc.vector.quantize_mx(
@@ -213,7 +205,8 @@ def tile_rbfnet_pb_k_kernel(
             return sm
 
         issue(LOOKAHEAD)
-        prepare(0, 2)
+        for first in range(0, FEAT_PASSES, GROUP):
+            prepare(first, GROUP)
         for blk in range(BLOCKS):
             s_bank = psum_wide.tile([P, BLOCK], F32, tag="wide", name="s_bank")
             nc.tensor.matmul(
@@ -225,11 +218,8 @@ def tile_rbfnet_pb_k_kernel(
 
         first_units = [(jt, blk * BLOCK, BLOCK) for jt in range(TEST_TILES) for blk in range(WIDE)]
         open_banks(psum_wide, "wide", first_units)
-        ahead = {1: (2, 2), 2: (4, 4), 4: (8, 4), 8: (12, 4)}
         for g in range(FEAT_PASSES):
             issue(g + LOOKAHEAD)
-            if g in ahead:
-                prepare(*ahead[g])
             for unit in first_units:
                 multiply(g, sm_tiles[g][:, unit[1] : unit[1] + BLOCK], unit)
 
@@ -254,7 +244,7 @@ def tile_rbfnet_pb_k_kernel(
         tiles = [narrow_load(narrow, "sm", first, STEP, n0, BLOCK) for first in range(0, SPLIT, STEP)]
         left = narrow_load(keep, "left", SPLIT, FEAT_PASSES - SPLIT, n0, HALF)
         right = narrow_load(keep, "right", SPLIT, FEAT_PASSES - SPLIT, n0 + HALF, HALF)
-        load_scales(y_planes, y_train_scales)
+        load_scales(nc.sync, I32, y_planes, y_train_scales)
         y_codes = keep.tile([P, BLOCKS, C], I32, align_bytes=256)
         nc.sync.dma_start(
             out=y_codes[:], in_=y_train_words.rearrange("g p n t -> p g (n t)").bitcast(I32)

@@ -33,8 +33,9 @@ QUAD_ORDER = (0, 2, 1, 3)
 WIDE = 2
 STEP = 2
 SPLIT = 8
-LOOKAHEAD = 10
-WARM = 16
+LOOKAHEAD = 6
+WARM_START, WARM_BETWEEN, WARM_END = 6, 2, 16
+X_PASSES = 8
 
 FLOPS = 2 * NTR * D * NTE + 2 * NTE * NTR * C
 
@@ -50,7 +51,8 @@ def tile_rbfnet_pb_k_kernel(
         narrow = stack.enter_context(tc.tile_pool(name="narrow", bufs=10))
         work = stack.enter_context(tc.tile_pool(name="work", bufs=4))
         psum_wide = stack.enter_context(tc.psum_pool(name="psum_wide", bufs=4))
-        psum_turn = stack.enter_context(tc.psum_pool(name="psum_turn", bufs=4))
+        psum_turn = stack.enter_context(tc.psum_pool(name="psum_turn", bufs=3))
+        psum_warm = stack.enter_context(tc.psum_pool(name="psum_warm", bufs=1))
         stack.enter_context(tc.manual_schedule())
 
         sm_planes = []
@@ -66,6 +68,8 @@ def tile_rbfnet_pb_k_kernel(
                     in_=source[:, quad * SCALE_ROWS : (quad + 1) * SCALE_ROWS, :].bitcast(dtype),
                 )
 
+        ones = keep.tile([P, BLOCK], BF16)
+        nc.vector.memset(ones[:], 1.0)
         ident_f32 = keep.tile([P, P], F32)
         make_identity(nc, ident_f32[:])
         s_row = keep.tile([P, NTR], BF16)
@@ -79,15 +83,13 @@ def tile_rbfnet_pb_k_kernel(
         c_bf16 = keep.tile([P, TEST_TILES], BF16)
         with nc.allow_non_contiguous_dma(reason="256 two-byte values, one to a partition"):
             nc.scalar.dma_start(out=c_bf16[:], in_=c_norm2.rearrange("(a p) -> p a", p=P))
-        ones = keep.tile([P, P], BF16)
-        nc.vector.memset(ones[:], 1.0)
         nc.gpsimd.memset(y_planes[:].bitcast(I32), 0)
         ident_bf16 = keep.tile([P, P], BF16)
         make_identity(nc, ident_bf16[:])
 
         x_raw = keep.tile([P, TEST_TILES, D], BF16)
         sm_tiles = {}
-        order = [("x", 0, 4), ("x", 4, 4), ("x", 8, 8)]
+        order = [("x", first, X_PASSES) for first in range(0, FEAT_PASSES, X_PASSES)]
         order += [("m", g, 1) for g in range(FEAT_PASSES)]
 
         def issue(last_pass):
@@ -112,28 +114,41 @@ def tile_rbfnet_pb_k_kernel(
                     )
 
         x_words = x_raw[:].bitcast(F32)
-        x_codes = keep.tile([P, FEAT_PASSES, NTE], U32, align_bytes=256)
-        x_planes = keep.tile([P, FEAT_PASSES, NTE], U8, align_bytes=256)
+        x_codes = keep.tile([P, TEST_TILES, FEAT_PASSES, P], U32, align_bytes=256)
+        x_planes = keep.tile([P, TEST_TILES, FEAT_PASSES, P], U8, align_bytes=256)
         half = K_PASS // 2
 
-        def prepare(first, count):
-            grouped = xstage.tile([P, count, TEST_TILES, P, PACK], BF16, align_bytes=256, tag="grouped", name="grouped")
-            grouped_words = grouped[:].bitcast(F32)
-            for i in range(count):
-                xt = psum_turn.tile([P, TEST_TILES, 2, P], F32, tag="turn", name="xt")
-                for jt in range(TEST_TILES):
+        runs, grouped = {}, {}
+
+        def reorder(jt, first):
+            runs[jt, first] = xstage.tile([P, X_PASSES, 2, P], F32, tag="runs", name="runs")
+            nc.vector.tensor_copy(
+                out=runs[jt, first][:],
+                in_=x_words[:, jt, first * half : (first + X_PASSES) * half].rearrange(
+                    "j (g p u) -> j g u p", g=X_PASSES, u=2
+                ),
+            )
+
+        def turn_words(jt, first):
+            grouped[jt, first] = xstage.tile(
+                [P, X_PASSES, P, PACK], BF16, align_bytes=256, tag="grouped", name="grouped"
+            )
+            grouped_words = grouped[jt, first][:].bitcast(F32)
+            for i in range(0, X_PASSES, 2):
+                xt = psum_turn.tile([P, 2, 2, P], F32, tag="turn", name="xt")
+                for g in range(2):
                     for u in range(2):
-                        word = (first + i) * half + u
-                        nc.tensor.transpose(
-                            xt[:, jt, u, :], x_words[:, jt, word : word + half - u : 2], ident_f32[:]
-                        )
-                copy = nc.vector.tensor_copy if i % 4 == 3 else nc.scalar.copy
-                copy(out=grouped_words[:, i], in_=xt[:].rearrange("p a u j -> p a j u"))
-            passes = slice(first, first + count)
+                        nc.tensor.transpose(xt[:, g, u, :], runs[jt, first][:, i + g, u, :], ident_f32[:])
+                nc.scalar.copy(
+                    out=grouped_words[:, i : i + 2], in_=xt[:].rearrange("p g u j -> p g j u")
+                )
+
+        def quantise_words(jt, first):
+            passes = slice(first, first + X_PASSES)
             nc.vector.quantize_mx(
-                out=x_codes[:, passes, :].rearrange("p g j -> p (g j)").bitcast(FP8X4),
-                scales=x_planes[:, passes, :].rearrange("p g j -> p (g j)"),
-                in_=grouped[:].rearrange("p g a j t -> p (g a j t)"),
+                out=x_codes[:, jt, passes, :].rearrange("p g j -> p (g j)").bitcast(FP8X4),
+                scales=x_planes[:, jt, passes, :].rearrange("p g j -> p (g j)"),
+                in_=grouped[jt, first][:].rearrange("p g j t -> p (g j t)"),
             )
 
         kern = keep.tile([P, TEST_TILES, BLOCKS, PACK, P], F32)
@@ -148,8 +163,8 @@ def tile_rbfnet_pb_k_kernel(
             a, b = divmod(g, GROUP)
             nc.tensor.matmul_mx(
                 out=acc[unit][:],
-                lhsT=x_codes[:, g, jt * P : (jt + 1) * P].bitcast(FP8X4),
-                lhsT_scale=x_planes[:, g, jt * P : (jt + 1) * P],
+                lhsT=x_codes[:, jt, g, :].bitcast(FP8X4),
+                lhsT_scale=x_planes[:, jt, g, :],
                 rhs=words.bitcast(FP8X4),
                 rhs_scale=sm_planes[a][b * SCALE_ROWS : P, n0 : n0 + n],
                 start=(g == 0),
@@ -204,22 +219,41 @@ def tile_rbfnet_pb_k_kernel(
             )
             return sm
 
+        def spread_s_norm2():
+            for blk in range(BLOCKS):
+                s_bank = psum_turn.tile([P, BLOCK], F32, tag="turn", name="s_bank")
+                nc.tensor.matmul(
+                    out=s_bank[:], lhsT=ones[:, :P], rhs=s_row[:, blk * BLOCK : (blk + 1) * BLOCK],
+                    start=True, stop=True,
+                )
+                nc.scalar.copy(out=s_all[:, blk], in_=s_bank[:].rearrange("p (q t) -> p t q", t=PACK))
+
         issue(LOOKAHEAD)
-        for first in range(0, FEAT_PASSES, GROUP):
-            prepare(first, GROUP)
-        for blk in range(BLOCKS):
-            s_bank = psum_wide.tile([P, BLOCK], F32, tag="wide", name="s_bank")
-            nc.tensor.matmul(
-                out=s_bank[:], lhsT=ones[:], rhs=s_row[:, blk * BLOCK : (blk + 1) * BLOCK],
-                start=True, stop=True,
-            )
-            nc.scalar.copy(out=s_all[:, blk], in_=s_bank[:].rearrange("p (q t) -> p t q", t=PACK))
-        nc.vector.tensor_copy(out=c_col[:], in_=c_bf16[:])
+        warm = psum_warm.tile([P, BLOCK], F32)
+
+        def keep_warm(count):
+            for i in range(count):
+                nc.tensor.matmul(out=warm[:], lhsT=ones[:, :P], rhs=ones[:], start=True, stop=True)
+
+        keep_warm(WARM_START)
+        x_pieces = [(jt, first) for first in range(0, FEAT_PASSES, X_PASSES) for jt in range(TEST_TILES)]
+        reorder(*x_pieces[0])
+        for n, piece in enumerate(x_pieces[:-1]):
+            turn_words(*piece)
+            reorder(*x_pieces[n + 1])
+            quantise_words(*piece)
+            keep_warm(WARM_BETWEEN)
 
         first_units = [(jt, blk * BLOCK, BLOCK) for jt in range(TEST_TILES) for blk in range(WIDE)]
         open_banks(psum_wide, "wide", first_units)
         for g in range(FEAT_PASSES):
             issue(g + LOOKAHEAD)
+            if g == 1:
+                turn_words(*x_pieces[-1])
+                quantise_words(*x_pieces[-1])
+            if g == FEAT_PASSES // 2:
+                spread_s_norm2()
+                nc.vector.tensor_copy(out=c_col[:], in_=c_bf16[:])
             for unit in first_units:
                 multiply(g, sm_tiles[g][:, unit[1] : unit[1] + BLOCK], unit)
 
@@ -249,7 +283,7 @@ def tile_rbfnet_pb_k_kernel(
         nc.sync.dma_start(
             out=y_codes[:], in_=y_train_words.rearrange("g p n t -> p g (n t)").bitcast(I32)
         )
-        open_banks(psum_turn, "turn", left_units)
+        open_banks(psum_wide, "wide", left_units)
         open_banks(psum_wide, "wide", right_units)
         for g in range(SPLIT):
             for jt in range(TEST_TILES):
@@ -273,9 +307,7 @@ def tile_rbfnet_pb_k_kernel(
                 root(unit)
         for jt in range(TEST_TILES):
             exponential(jt, BLOCKS - 1, last_d2[:, jt])
-        warm = psum_turn.tile([P, BLOCK], F32, tag="turn", name="warm")
-        for i in range(WARM):
-            nc.tensor.matmul(out=warm[:], lhsT=ones[:], rhs=s_row[:, :BLOCK], start=True, stop=True)
+        keep_warm(WARM_END)
 
         total = keep.tile([P, TEST_TILES], F32)
         rsum = keep.tile([P, TEST_TILES], F32)

@@ -32,9 +32,8 @@ LIVE = GROUP * SCALE_ROWS
 QUAD_ORDER = (0, 2, 1, 3)
 WIDE = 2
 STEP = 2
-SPLIT = 8
 LOOKAHEAD = 6
-WARM_START, WARM_BETWEEN, WARM_END = 6, 2, 16
+WARM_START, WARM_BETWEEN, WARM_END = 6, 2, 8
 X_PASSES = 8
 
 FLOPS = 2 * NTR * D * NTE + 2 * NTE * NTR * C
@@ -50,9 +49,9 @@ def tile_rbfnet_pb_k_kernel(
         stream = stack.enter_context(tc.tile_pool(name="stream", bufs=LOOKAHEAD + 2))
         narrow = stack.enter_context(tc.tile_pool(name="narrow", bufs=10))
         work = stack.enter_context(tc.tile_pool(name="work", bufs=4))
+        weights = stack.enter_context(tc.tile_pool(name="weights", bufs=8))
         psum_wide = stack.enter_context(tc.psum_pool(name="psum_wide", bufs=4))
-        psum_turn = stack.enter_context(tc.psum_pool(name="psum_turn", bufs=3))
-        psum_warm = stack.enter_context(tc.psum_pool(name="psum_warm", bufs=1))
+        psum_turn = stack.enter_context(tc.psum_pool(name="psum_turn", bufs=4))
         stack.enter_context(tc.manual_schedule())
 
         sm_planes = []
@@ -68,18 +67,17 @@ def tile_rbfnet_pb_k_kernel(
                     in_=source[:, quad * SCALE_ROWS : (quad + 1) * SCALE_ROWS, :].bitcast(dtype),
                 )
 
+        s_row = keep.tile([P, NTR], BF16)
+        nc.vector.memset(s_row[:].bitcast(I32), 0)
         ones = keep.tile([P, BLOCK], BF16)
         nc.vector.memset(ones[:], 1.0)
         ident_f32 = keep.tile([P, P], F32)
         make_identity(nc, ident_f32[:])
-        s_row = keep.tile([P, NTR], BF16)
         nc.vector.memset(sm_planes[0][:].bitcast(I32), 0)
-        nc.vector.memset(s_row[:].bitcast(I32), 0)
         for a in range(GROUPS):
             if a > 0:
                 nc.vector.memset(sm_planes[a][:].bitcast(I32), 0)
-            load_scales(nc.gpsimd, F32, sm_planes[a], sM_scales[a * GROUP : (a + 1) * GROUP])
-        nc.scalar.dma_start(out=s_row[0:1, :], in_=s_norm2.rearrange("(o n) -> o n", o=1))
+                load_scales(nc.gpsimd, F32, sm_planes[a], sM_scales[a * GROUP : (a + 1) * GROUP])
         c_bf16 = keep.tile([P, TEST_TILES], BF16)
         with nc.allow_non_contiguous_dma(reason="256 two-byte values, one to a partition"):
             nc.scalar.dma_start(out=c_bf16[:], in_=c_norm2.rearrange("(a p) -> p a", p=P))
@@ -89,14 +87,17 @@ def tile_rbfnet_pb_k_kernel(
 
         x_raw = keep.tile([P, TEST_TILES, D], BF16)
         sm_tiles = {}
-        order = [("x", first, X_PASSES) for first in range(0, FEAT_PASSES, X_PASSES)]
+        order = [("x", 0, X_PASSES), ("s", 0, 0), ("x", X_PASSES, X_PASSES)]
         order += [("m", g, 1) for g in range(FEAT_PASSES)]
 
         def issue(last_pass):
             while order and (order[0][0] != "m" or order[0][1] <= last_pass):
                 kind, first, count = order[0]
                 order.remove(order[0])
-                if kind == "x":
+                if kind == "s":
+                    nc.sync.dma_start(out=s_row[0:1, :], in_=s_norm2.rearrange("(o n) -> o n", o=1))
+                    load_scales(nc.sync, I32, sm_planes[0], sM_scales[:GROUP])
+                elif kind == "x":
                     cols = slice(first * K_PASS, (first + count) * K_PASS)
                     for jt in range(TEST_TILES):
                         nc.sync.dma_start(
@@ -138,8 +139,14 @@ def tile_rbfnet_pb_k_kernel(
                 xt = psum_turn.tile([P, 2, 2, P], F32, tag="turn", name="xt")
                 for g in range(2):
                     for u in range(2):
-                        nc.tensor.transpose(xt[:, g, u, :], runs[jt, first][:, i + g, u, :], ident_f32[:])
-                nc.scalar.copy(
+                        word = (first + i + g) * half + u
+                        if (jt, first) in runs:
+                            words = runs[jt, first][:, i + g, u, :]
+                        else:
+                            words = x_words[:, jt, word : word + half - u : 2]
+                        nc.tensor.transpose(xt[:, g, u, :], words, ident_f32[:])
+                copy = nc.vector.tensor_copy if i == X_PASSES - 2 else nc.scalar.copy
+                copy(
                     out=grouped_words[:, i : i + 2], in_=xt[:].rearrange("p g u j -> p g j u")
                 )
 
@@ -153,7 +160,7 @@ def tile_rbfnet_pb_k_kernel(
 
         kern = keep.tile([P, TEST_TILES, BLOCKS, PACK, P], F32)
         ksum = keep.tile([P, TEST_TILES, BLOCKS], F32)
-        last_d2 = keep.tile([P, TEST_TILES, PACK, P], F32)
+        last_d2 = keep.tile([P, PACK, P], F32)
         s_all = keep.tile([P, BLOCKS, PACK, P], BF16)
         c_col = keep.tile([P, TEST_TILES], F32)
         acc, d2 = {}, {}
@@ -182,7 +189,7 @@ def tile_rbfnet_pb_k_kernel(
                 whole = work.tile([P, PACK, P], F32, tag="d2", name="d2")
                 d2[unit] = whole[:]
             else:
-                d2[unit] = place(last_d2[:, jt], unit)
+                d2[unit] = place(last_d2[:], unit)
             nc.vector.scalar_tensor_tensor(
                 out=d2[unit],
                 in0=acc[unit][:].rearrange("p (q t) -> p t q", t=PACK),
@@ -205,12 +212,17 @@ def tile_rbfnet_pb_k_kernel(
                 scale=-1.0 / GAMMA, accum_out=ksum[:, jt, blk : blk + 1],
             )
 
+        spare = keep.tile([P, 1], F32)
+
+        def load_root_table():
+            nc.scalar.activation(out=spare[:], in_=ksum[:, 0, 0:1], func=ACT.Sqrt)
+
         def open_banks(pool, tag, units):
             for unit in units:
                 acc[unit] = pool.tile([P, unit[2]], F32, tag=tag, name="acc_%d_%d" % unit[:2])
 
-        def narrow_load(pool, tag, first, passes, n0, n):
-            sm = pool.tile([P, passes, n], I32, align_bytes=256, tag=tag, name="sm")
+        def narrow_load(first, passes, n0, n):
+            sm = narrow.tile([P, passes, n], I32, align_bytes=256, tag="sm", name="sm")
             nc.sync.dma_start(
                 out=sm[:],
                 in_=sM_words[first : first + passes, :, n0 : n0 + n, :]
@@ -229,37 +241,40 @@ def tile_rbfnet_pb_k_kernel(
                 nc.scalar.copy(out=s_all[:, blk], in_=s_bank[:].rearrange("p (q t) -> p t q", t=PACK))
 
         issue(LOOKAHEAD)
-        warm = psum_warm.tile([P, BLOCK], F32)
 
         def keep_warm(count):
+            warm = psum_wide.tile([P, BLOCK], F32, tag="wide", name="warm")
             for i in range(count):
                 nc.tensor.matmul(out=warm[:], lhsT=ones[:, :P], rhs=ones[:], start=True, stop=True)
 
         keep_warm(WARM_START)
         x_pieces = [(jt, first) for first in range(0, FEAT_PASSES, X_PASSES) for jt in range(TEST_TILES)]
         reorder(*x_pieces[0])
-        for n, piece in enumerate(x_pieces[:-1]):
-            turn_words(*piece)
-            reorder(*x_pieces[n + 1])
-            quantise_words(*piece)
-            keep_warm(WARM_BETWEEN)
+
+        def make_ready(n):
+            turn_words(*x_pieces[n])
+            quantise_words(*x_pieces[n])
+
+        make_ready(0)
+        keep_warm(WARM_BETWEEN)
+        make_ready(1)
+        spread_s_norm2()
+        make_ready(2)
+        reorder(*x_pieces[3])
 
         first_units = [(jt, blk * BLOCK, BLOCK) for jt in range(TEST_TILES) for blk in range(WIDE)]
         open_banks(psum_wide, "wide", first_units)
         for g in range(FEAT_PASSES):
             issue(g + LOOKAHEAD)
-            if g == 1:
-                turn_words(*x_pieces[-1])
-                quantise_words(*x_pieces[-1])
-            if g == FEAT_PASSES // 2:
-                spread_s_norm2()
+            if g == 3:
+                make_ready(3)
                 nc.vector.tensor_copy(out=c_col[:], in_=c_bf16[:])
             for unit in first_units:
                 multiply(g, sm_tiles[g][:, unit[1] : unit[1] + BLOCK], unit)
 
         n0 = WIDE * BLOCK
         second_units = [(jt, n0, BLOCK) for jt in range(TEST_TILES)]
-        tiles = [narrow_load(narrow, "sm", first, STEP, n0, BLOCK) for first in range(0, FEAT_PASSES, STEP)]
+        tiles = [narrow_load(first, STEP, n0, BLOCK) for first in range(0, FEAT_PASSES, STEP)]
         open_banks(psum_turn, "turn", second_units)
         for first in range(0, FEAT_PASSES, STEP):
             for unit in second_units:
@@ -271,51 +286,23 @@ def tile_rbfnet_pb_k_kernel(
             root(unit)
         for unit in first_units:
             exponential(unit[0], unit[1] // BLOCK, d2[unit])
+        load_root_table()
 
         n0 = (BLOCKS - 1) * BLOCK
-        left_units = [(jt, n0, HALF) for jt in range(TEST_TILES)]
-        right_units = [(jt, n0 + HALF, HALF) for jt in range(TEST_TILES)]
-        tiles = [narrow_load(narrow, "sm", first, STEP, n0, BLOCK) for first in range(0, SPLIT, STEP)]
-        left = narrow_load(keep, "left", SPLIT, FEAT_PASSES - SPLIT, n0, HALF)
-        right = narrow_load(keep, "right", SPLIT, FEAT_PASSES - SPLIT, n0 + HALF, HALF)
+        third_unit = (0, n0, BLOCK)
+        half_units = [(1, n0, HALF), (1, n0 + HALF, HALF)]
+        tiles = [narrow_load(first, STEP, n0, BLOCK) for first in range(0, FEAT_PASSES, STEP)]
         load_scales(nc.sync, I32, y_planes, y_train_scales)
         y_codes = keep.tile([P, BLOCKS, C], I32, align_bytes=256)
         nc.sync.dma_start(
             out=y_codes[:], in_=y_train_words.rearrange("g p n t -> p g (n t)").bitcast(I32)
         )
-        open_banks(psum_wide, "wide", left_units)
-        open_banks(psum_wide, "wide", right_units)
-        for g in range(SPLIT):
-            for jt in range(TEST_TILES):
-                multiply(g, tiles[g // STEP][:, g % STEP, :HALF], left_units[jt])
-                multiply(g, tiles[g // STEP][:, g % STEP, HALF:], right_units[jt])
-        for unit in second_units:
-            squared_distance(unit)
-        spare = keep.tile([P, 1], F32)
-        for unit in second_units:
-            root(unit)
-        for unit in second_units:
-            exponential(unit[0], unit[1] // BLOCK, d2[unit])
-        nc.scalar.activation(out=spare[:], in_=ksum[:, 0, 0:1], func=ACT.Sqrt)
-        for words, units in ((left, left_units), (right, right_units)):
-            for unit in units:
-                for g in range(SPLIT, FEAT_PASSES):
-                    multiply(g, words[:, g - SPLIT, :], unit)
-            for unit in units:
-                squared_distance(unit)
-            for unit in units:
-                root(unit)
-        for jt in range(TEST_TILES):
-            exponential(jt, BLOCKS - 1, last_d2[:, jt])
-        keep_warm(WARM_END)
-
+        open_banks(psum_wide, "wide", [third_unit] + half_units)
         total = keep.tile([P, TEST_TILES], F32)
         rsum = keep.tile([P, TEST_TILES], F32)
         w_codes = keep.tile([P, TEST_TILES, BLOCKS, P], U32, align_bytes=256)
         w_planes = keep.tile([P, TEST_TILES, BLOCKS, P], U8, align_bytes=256)
-        pieces = [(jt, blk) for jt in range(TEST_TILES) for blk in range(BLOCKS)]
-        on_scalar = [(1, 0), (1, 1)]
-        w_bf16, w_grouped, o_bank = {}, {}, {}
+        w_bf16, turned, w_grouped, o_bank = {}, {}, {}, {}
 
         def reciprocal_sum(jt):
             nc.vector.tensor_reduce(
@@ -323,10 +310,10 @@ def tile_rbfnet_pb_k_kernel(
             )
             nc.vector.reciprocal(out=rsum[:, jt : jt + 1], in_=total[:, jt : jt + 1])
 
-        def normalise(piece):
+        def normalise(piece, on_scalar=False):
             jt, blk = piece
-            w_bf16[piece] = work.tile([P, PACK, P], BF16, tag="w_bf16", name="w_bf16")
-            if piece in on_scalar:
+            w_bf16[piece] = weights.tile([P, PACK, P], BF16, tag="w_bf16", name="w_bf16")
+            if on_scalar:
                 nc.scalar.activation(
                     out=w_bf16[piece][:], in_=kern[:, jt, blk], func=ACT.Copy, scale=rsum[:, jt : jt + 1]
                 )
@@ -337,14 +324,13 @@ def tile_rbfnet_pb_k_kernel(
                 )
 
         def turn(piece):
-            if piece == pieces[1]:
-                for other in on_scalar:
-                    normalise(other)
-            wt = psum_wide.tile([P, PACK, P], BF16, tag="wide", name="wt")
+            turned[piece] = psum_wide.tile([P, PACK, P], BF16, tag="wide", name="turned")
             for t in range(PACK):
-                nc.tensor.transpose(wt[:, t, :], w_bf16[piece][:, t, :], ident_bf16[:])
-            w_grouped[piece] = work.tile([P, P, PACK], BF16, align_bytes=256, tag="w_grouped", name="w_grouped")
-            nc.scalar.copy(out=w_grouped[piece][:], in_=wt[:].rearrange("p t j -> p j t"))
+                nc.tensor.transpose(turned[piece][:, t, :], w_bf16[piece][:, t, :], ident_bf16[:])
+
+        def regroup(piece, copy):
+            w_grouped[piece] = weights.tile([P, P, PACK], BF16, align_bytes=256, tag="w_grouped", name="w_grouped")
+            copy(out=w_grouped[piece][:], in_=turned[piece][:].rearrange("p t j -> p j t"))
 
         def quantise(piece):
             jt, blk = piece
@@ -354,34 +340,64 @@ def tile_rbfnet_pb_k_kernel(
                 in_=w_grouped[piece][:].rearrange("p j t -> p (j t)"),
             )
 
-        def second_product(piece):
-            jt, blk = piece
-            if blk == 0:
-                o_bank[jt] = psum_turn.tile([P, C], F32, tag="turn", name="o_bank")
-            nc.tensor.matmul_mx(
-                out=o_bank[jt][:],
-                lhsT=w_codes[:, jt, blk, :].bitcast(FP8X4),
-                lhsT_scale=w_planes[:, jt, blk, :],
-                rhs=y_codes[:, blk, :].bitcast(FP8X4),
-                rhs_scale=y_planes[blk * SCALE_ROWS : P, :],
-                start=(blk == 0),
-                stop=(blk == BLOCKS - 1),
-            )
-            if blk == BLOCKS - 1:
-                result = work.tile([P, C], F32, name="result")
-                nc.vector.tensor_copy(out=result[:], in_=o_bank[jt][:])
-                nc.sync.dma_start(out=out[jt * P : (jt + 1) * P, :], in_=result[:])
+        def second_product(jt):
+            o_bank[jt] = psum_turn.tile([P, C], F32, tag="turn", name="o_bank")
+            for blk in range(BLOCKS):
+                nc.tensor.matmul_mx(
+                    out=o_bank[jt][:],
+                    lhsT=w_codes[:, jt, blk, :].bitcast(FP8X4),
+                    lhsT_scale=w_planes[:, jt, blk, :],
+                    rhs=y_codes[:, blk, :].bitcast(FP8X4),
+                    rhs_scale=y_planes[blk * SCALE_ROWS : P, :],
+                    start=(blk == 0),
+                    stop=(blk == BLOCKS - 1),
+                )
 
+        def store(jt, copy):
+            result = weights.tile([P, C], F32, tag="result", name="result")
+            copy(out=result[:], in_=o_bank[jt][:])
+            nc.sync.dma_start(out=out[jt * P : (jt + 1) * P, :], in_=result[:])
+
+        for unit in second_units:
+            squared_distance(unit)
+        for unit in second_units:
+            root(unit)
+        for g in range(FEAT_PASSES):
+            multiply(g, tiles[g // STEP][:, g % STEP, :], third_unit)
+        squared_distance(third_unit)
+        root(third_unit)
+        for unit in [third_unit] + second_units:
+            exponential(unit[0], unit[1] // BLOCK, d2[unit])
+        for h, unit in enumerate(half_units):
+            for g in range(FEAT_PASSES):
+                multiply(g, tiles[g // STEP][:, g % STEP, h * HALF : (h + 1) * HALF], unit)
+        squared_distance(half_units[0])
         reciprocal_sum(0)
-        lag, depth = 3, 5
-        for n in range(len(pieces) + depth):
-            if n == 1:
-                reciprocal_sum(1)
-            if n < len(pieces):
-                if pieces[n] not in on_scalar:
-                    normalise(pieces[n])
-                turn(pieces[n])
-            if lag <= n < len(pieces) + lag:
-                quantise(pieces[n - lag])
-            if n >= depth:
-                second_product(pieces[n - depth])
+        normalise((0, 0))
+        squared_distance(half_units[1])
+        load_root_table()
+        for unit in half_units:
+            root(unit)
+        exponential(1, BLOCKS - 1, last_d2[:])
+        for blk in range(1, BLOCKS):
+            normalise((0, blk))
+        keep_warm(WARM_BETWEEN)
+        for blk in range(BLOCKS):
+            turn((0, blk))
+        keep_warm(WARM_END)
+        for blk in range(BLOCKS):
+            regroup((0, blk), nc.vector.tensor_copy)
+        for blk in range(BLOCKS):
+            quantise((0, blk))
+        second_product(0)
+        store(0, nc.scalar.copy)
+        reciprocal_sum(1)
+        for blk in range(BLOCKS):
+            normalise((1, blk), on_scalar=blk == 2)
+            turn((1, blk))
+        for blk in range(BLOCKS):
+            regroup((1, blk), nc.scalar.copy)
+        for blk in range(BLOCKS):
+            quantise((1, blk))
+        second_product(1)
+        store(1, nc.vector.tensor_copy)

@@ -33,7 +33,9 @@ QUAD_ORDER = (0, 2, 1, 3)
 WIDE = 2
 STEP = 2
 LOOKAHEAD = 6
-WARM_START, WARM_BETWEEN, WARM_END = 6, 2, 8
+WARM_START, WARM_BETWEEN, WARM_END = 6, 2, 16
+SPLIT = 8
+CHUNK = 4
 X_PASSES = 8
 
 FLOPS = 2 * NTR * D * NTE + 2 * NTE * NTR * C
@@ -47,9 +49,8 @@ def tile_rbfnet_pb_k_kernel(
         keep = stack.enter_context(tc.tile_pool(name="keep", bufs=1))
         xstage = stack.enter_context(tc.tile_pool(name="xstage", bufs=2))
         stream = stack.enter_context(tc.tile_pool(name="stream", bufs=LOOKAHEAD + 2))
-        narrow = stack.enter_context(tc.tile_pool(name="narrow", bufs=10))
+        narrow = stack.enter_context(tc.tile_pool(name="narrow", bufs=9))
         work = stack.enter_context(tc.tile_pool(name="work", bufs=4))
-        weights = stack.enter_context(tc.tile_pool(name="weights", bufs=8))
         psum_wide = stack.enter_context(tc.psum_pool(name="psum_wide", bufs=4))
         psum_turn = stack.enter_context(tc.psum_pool(name="psum_turn", bufs=4))
         stack.enter_context(tc.manual_schedule())
@@ -139,12 +140,7 @@ def tile_rbfnet_pb_k_kernel(
                 xt = psum_turn.tile([P, 2, 2, P], F32, tag="turn", name="xt")
                 for g in range(2):
                     for u in range(2):
-                        word = (first + i + g) * half + u
-                        if (jt, first) in runs:
-                            words = runs[jt, first][:, i + g, u, :]
-                        else:
-                            words = x_words[:, jt, word : word + half - u : 2]
-                        nc.tensor.transpose(xt[:, g, u, :], words, ident_f32[:])
+                        nc.tensor.transpose(xt[:, g, u, :], runs[jt, first][:, i + g, u, :], ident_f32[:])
                 copy = nc.vector.tensor_copy if i == X_PASSES - 2 else nc.scalar.copy
                 copy(
                     out=grouped_words[:, i : i + 2], in_=xt[:].rearrange("p g u j -> p g j u")
@@ -160,7 +156,7 @@ def tile_rbfnet_pb_k_kernel(
 
         kern = keep.tile([P, TEST_TILES, BLOCKS, PACK, P], F32)
         ksum = keep.tile([P, TEST_TILES, BLOCKS], F32)
-        last_d2 = keep.tile([P, PACK, P], F32)
+        last_d2 = keep.tile([P, TEST_TILES, PACK, P], F32)
         s_all = keep.tile([P, BLOCKS, PACK, P], BF16)
         c_col = keep.tile([P, TEST_TILES], F32)
         acc, d2 = {}, {}
@@ -189,7 +185,7 @@ def tile_rbfnet_pb_k_kernel(
                 whole = work.tile([P, PACK, P], F32, tag="d2", name="d2")
                 d2[unit] = whole[:]
             else:
-                d2[unit] = place(last_d2[:], unit)
+                d2[unit] = place(last_d2[:, jt], unit)
             nc.vector.scalar_tensor_tensor(
                 out=d2[unit],
                 in0=acc[unit][:].rearrange("p (q t) -> p t q", t=PACK),
@@ -221,8 +217,8 @@ def tile_rbfnet_pb_k_kernel(
             for unit in units:
                 acc[unit] = pool.tile([P, unit[2]], F32, tag=tag, name="acc_%d_%d" % unit[:2])
 
-        def narrow_load(first, passes, n0, n):
-            sm = narrow.tile([P, passes, n], I32, align_bytes=256, tag="sm", name="sm")
+        def narrow_load(pool, tag, first, passes, n0, n):
+            sm = pool.tile([P, passes, n], I32, align_bytes=256, tag=tag, name="sm")
             nc.sync.dma_start(
                 out=sm[:],
                 in_=sM_words[first : first + passes, :, n0 : n0 + n, :]
@@ -250,17 +246,19 @@ def tile_rbfnet_pb_k_kernel(
         keep_warm(WARM_START)
         x_pieces = [(jt, first) for first in range(0, FEAT_PASSES, X_PASSES) for jt in range(TEST_TILES)]
         reorder(*x_pieces[0])
+        reorder(*x_pieces[1])
 
         def make_ready(n):
             turn_words(*x_pieces[n])
             quantise_words(*x_pieces[n])
+            if n + 2 < len(x_pieces):
+                reorder(*x_pieces[n + 2])
 
         make_ready(0)
         keep_warm(WARM_BETWEEN)
         make_ready(1)
         spread_s_norm2()
         make_ready(2)
-        reorder(*x_pieces[3])
 
         first_units = [(jt, blk * BLOCK, BLOCK) for jt in range(TEST_TILES) for blk in range(WIDE)]
         open_banks(psum_wide, "wide", first_units)
@@ -274,7 +272,7 @@ def tile_rbfnet_pb_k_kernel(
 
         n0 = WIDE * BLOCK
         second_units = [(jt, n0, BLOCK) for jt in range(TEST_TILES)]
-        tiles = [narrow_load(first, STEP, n0, BLOCK) for first in range(0, FEAT_PASSES, STEP)]
+        tiles = [narrow_load(narrow, "sm", first, STEP, n0, BLOCK) for first in range(0, FEAT_PASSES, STEP)]
         open_banks(psum_turn, "turn", second_units)
         for first in range(0, FEAT_PASSES, STEP):
             for unit in second_units:
@@ -289,20 +287,52 @@ def tile_rbfnet_pb_k_kernel(
         load_root_table()
 
         n0 = (BLOCKS - 1) * BLOCK
-        third_unit = (0, n0, BLOCK)
-        half_units = [(1, n0, HALF), (1, n0 + HALF, HALF)]
-        tiles = [narrow_load(first, STEP, n0, BLOCK) for first in range(0, FEAT_PASSES, STEP)]
+        left_units = [(jt, n0, HALF) for jt in range(TEST_TILES)]
+        right_units = [(jt, n0 + HALF, HALF) for jt in range(TEST_TILES)]
+        tiles = [narrow_load(narrow, "sm", first, STEP, n0, BLOCK) for first in range(0, SPLIT, STEP)]
+        ends = [
+            [narrow_load(keep, "end_%d_%d" % (h, first), first, CHUNK, n0 + h * HALF, HALF)
+             for first in range(SPLIT, FEAT_PASSES, CHUNK)]
+            for h in range(2)
+        ]
         load_scales(nc.sync, I32, y_planes, y_train_scales)
         y_codes = keep.tile([P, BLOCKS, C], I32, align_bytes=256)
         nc.sync.dma_start(
             out=y_codes[:], in_=y_train_words.rearrange("g p n t -> p g (n t)").bitcast(I32)
         )
-        open_banks(psum_wide, "wide", [third_unit] + half_units)
+        open_banks(psum_wide, "wide", left_units)
+        open_banks(psum_wide, "wide", right_units)
+        for g in range(SPLIT):
+            for jt in range(TEST_TILES):
+                multiply(g, tiles[g // STEP][:, g % STEP, :HALF], left_units[jt])
+                multiply(g, tiles[g // STEP][:, g % STEP, HALF:], right_units[jt])
+        for unit in second_units:
+            squared_distance(unit)
+        for unit in second_units:
+            root(unit)
+        for unit in second_units:
+            exponential(unit[0], unit[1] // BLOCK, d2[unit])
+        load_root_table()
+        for words, units in zip(ends, (left_units, right_units)):
+            for first in range(SPLIT, FEAT_PASSES, CHUNK):
+                for unit in units:
+                    for i in range(CHUNK):
+                        multiply(first + i, words[(first - SPLIT) // CHUNK][:, i, :], unit)
+            for unit in units:
+                squared_distance(unit)
+            for unit in units:
+                root(unit)
+        for jt in range(TEST_TILES):
+            exponential(jt, BLOCKS - 1, last_d2[:, jt])
+        keep_warm(WARM_END)
+
         total = keep.tile([P, TEST_TILES], F32)
         rsum = keep.tile([P, TEST_TILES], F32)
         w_codes = keep.tile([P, TEST_TILES, BLOCKS, P], U32, align_bytes=256)
         w_planes = keep.tile([P, TEST_TILES, BLOCKS, P], U8, align_bytes=256)
-        w_bf16, turned, w_grouped, o_bank = {}, {}, {}, {}
+        pieces = [(jt, blk) for jt in range(TEST_TILES) for blk in range(BLOCKS)]
+        on_scalar = (1, 0)
+        w_bf16, w_grouped, o_bank = {}, {}, {}
 
         def reciprocal_sum(jt):
             nc.vector.tensor_reduce(
@@ -310,10 +340,10 @@ def tile_rbfnet_pb_k_kernel(
             )
             nc.vector.reciprocal(out=rsum[:, jt : jt + 1], in_=total[:, jt : jt + 1])
 
-        def normalise(piece, on_scalar=False):
+        def normalise(piece):
             jt, blk = piece
-            w_bf16[piece] = weights.tile([P, PACK, P], BF16, tag="w_bf16", name="w_bf16")
-            if on_scalar:
+            w_bf16[piece] = work.tile([P, PACK, P], BF16, tag="w_bf16", name="w_bf16")
+            if piece == on_scalar:
                 nc.scalar.activation(
                     out=w_bf16[piece][:], in_=kern[:, jt, blk], func=ACT.Copy, scale=rsum[:, jt : jt + 1]
                 )
@@ -324,80 +354,62 @@ def tile_rbfnet_pb_k_kernel(
                 )
 
         def turn(piece):
-            turned[piece] = psum_wide.tile([P, PACK, P], BF16, tag="wide", name="turned")
+            wt = psum_wide.tile([P, PACK, P], BF16, tag="wide", name="wt")
             for t in range(PACK):
-                nc.tensor.transpose(turned[piece][:, t, :], w_bf16[piece][:, t, :], ident_bf16[:])
-
-        def regroup(piece, copy):
-            w_grouped[piece] = weights.tile([P, P, PACK], BF16, align_bytes=256, tag="w_grouped", name="w_grouped")
-            copy(out=w_grouped[piece][:], in_=turned[piece][:].rearrange("p t j -> p j t"))
-
-        def quantise(piece):
+                nc.tensor.transpose(wt[:, t, :], w_bf16[piece][:, t, :], ident_bf16[:])
             jt, blk = piece
-            nc.vector.quantize_mx(
-                out=w_codes[:, jt, blk, :].bitcast(FP8X4),
-                scales=w_planes[:, jt, blk, :],
-                in_=w_grouped[piece][:].rearrange("p j t -> p (j t)"),
+            if blk % 2 == 0:
+                w_grouped[jt, blk // 2] = work.tile(
+                    [P, 2, P, PACK], BF16, align_bytes=256, tag="w_grouped", name="w_grouped"
+                )
+            nc.scalar.copy(
+                out=w_grouped[jt, blk // 2][:, blk % 2], in_=wt[:].rearrange("p t j -> p j t")
             )
 
-        def second_product(jt):
-            o_bank[jt] = psum_turn.tile([P, C], F32, tag="turn", name="o_bank")
-            for blk in range(BLOCKS):
-                nc.tensor.matmul_mx(
-                    out=o_bank[jt][:],
-                    lhsT=w_codes[:, jt, blk, :].bitcast(FP8X4),
-                    lhsT_scale=w_planes[:, jt, blk, :],
-                    rhs=y_codes[:, blk, :].bitcast(FP8X4),
-                    rhs_scale=y_planes[blk * SCALE_ROWS : P, :],
-                    start=(blk == 0),
-                    stop=(blk == BLOCKS - 1),
-                )
+        def quantise(jt, first, count):
+            half, inner = divmod(first, 2)
+            blocks = slice(first, first + count)
+            nc.vector.quantize_mx(
+                out=w_codes[:, jt, blocks, :].rearrange("p b j -> p (b j)").bitcast(FP8X4),
+                scales=w_planes[:, jt, blocks, :].rearrange("p b j -> p (b j)"),
+                in_=w_grouped[jt, half][:, inner : inner + count].rearrange("p b j t -> p (b j t)"),
+            )
 
-        def store(jt, copy):
-            result = weights.tile([P, C], F32, tag="result", name="result")
-            copy(out=result[:], in_=o_bank[jt][:])
-            nc.sync.dma_start(out=out[jt * P : (jt + 1) * P, :], in_=result[:])
+        def second_product(piece):
+            jt, blk = piece
+            if blk == 0:
+                o_bank[jt] = psum_turn.tile([P, C], F32, tag="turn", name="o_bank")
+            nc.tensor.matmul_mx(
+                out=o_bank[jt][:],
+                lhsT=w_codes[:, jt, blk, :].bitcast(FP8X4),
+                lhsT_scale=w_planes[:, jt, blk, :],
+                rhs=y_codes[:, blk, :].bitcast(FP8X4),
+                rhs_scale=y_planes[blk * SCALE_ROWS : P, :],
+                start=(blk == 0),
+                stop=(blk == BLOCKS - 1),
+            )
+            if blk == BLOCKS - 1:
+                result = work.tile([P, C], F32, name="result")
+                copy = nc.scalar.copy if jt == 0 else nc.vector.tensor_copy
+                copy(out=result[:], in_=o_bank[jt][:])
+                nc.sync.dma_start(out=out[jt * P : (jt + 1) * P, :], in_=result[:])
 
-        for unit in second_units:
-            squared_distance(unit)
-        for unit in second_units:
-            root(unit)
-        for g in range(FEAT_PASSES):
-            multiply(g, tiles[g // STEP][:, g % STEP, :], third_unit)
-        squared_distance(third_unit)
-        root(third_unit)
-        for unit in [third_unit] + second_units:
-            exponential(unit[0], unit[1] // BLOCK, d2[unit])
-        for h, unit in enumerate(half_units):
-            for g in range(FEAT_PASSES):
-                multiply(g, tiles[g // STEP][:, g % STEP, h * HALF : (h + 1) * HALF], unit)
-        squared_distance(half_units[0])
         reciprocal_sum(0)
-        normalise((0, 0))
-        squared_distance(half_units[1])
-        load_root_table()
-        for unit in half_units:
-            root(unit)
-        exponential(1, BLOCKS - 1, last_d2[:])
-        for blk in range(1, BLOCKS):
-            normalise((0, blk))
-        keep_warm(WARM_BETWEEN)
-        for blk in range(BLOCKS):
-            turn((0, blk))
-        keep_warm(WARM_END)
-        for blk in range(BLOCKS):
-            regroup((0, blk), nc.vector.tensor_copy)
-        for blk in range(BLOCKS):
-            quantise((0, blk))
-        second_product(0)
-        store(0, nc.scalar.copy)
-        reciprocal_sum(1)
-        for blk in range(BLOCKS):
-            normalise((1, blk), on_scalar=blk == 2)
-            turn((1, blk))
-        for blk in range(BLOCKS):
-            regroup((1, blk), nc.scalar.copy)
-        for blk in range(BLOCKS):
-            quantise((1, blk))
-        second_product(1)
-        store(1, nc.vector.tensor_copy)
+        for n, piece in enumerate(pieces):
+            if n == 1:
+                reciprocal_sum(1)
+            if n == 2:
+                normalise(on_scalar)
+            if piece != on_scalar:
+                normalise(piece)
+            turn(piece)
+            if n == BLOCKS - 1:
+                quantise(0, 0, 2)
+        quantise(0, 2, 2)
+        quantise(1, 0, 2)
+        for piece in pieces[:BLOCKS]:
+            second_product(piece)
+        for piece in pieces[BLOCKS:]:
+            if piece[1] >= 2:
+                quantise(*piece, 1)
+            second_product(piece)

@@ -68,17 +68,17 @@ def tile_rbfnet_pb_k_kernel(
                     in_=source[:, quad * SCALE_ROWS : (quad + 1) * SCALE_ROWS, :].bitcast(dtype),
                 )
 
-        s_row = keep.tile([P, NTR], BF16)
-        nc.vector.memset(s_row[:].bitcast(I32), 0)
+        nc.vector.memset(sm_planes[0][:].bitcast(I32), 0)
         ones = keep.tile([P, BLOCK], BF16)
         nc.vector.memset(ones[:], 1.0)
+        s_row = keep.tile([P, NTR], BF16)
+        nc.vector.memset(s_row[:].bitcast(I32), 0)
         ident_f32 = keep.tile([P, P], F32)
         make_identity(nc, ident_f32[:])
-        nc.vector.memset(sm_planes[0][:].bitcast(I32), 0)
         for a in range(GROUPS):
             if a > 0:
                 nc.vector.memset(sm_planes[a][:].bitcast(I32), 0)
-                load_scales(nc.gpsimd, F32, sm_planes[a], sM_scales[a * GROUP : (a + 1) * GROUP])
+            load_scales(nc.gpsimd, F32, sm_planes[a], sM_scales[a * GROUP : (a + 1) * GROUP])
         c_bf16 = keep.tile([P, TEST_TILES], BF16)
         with nc.allow_non_contiguous_dma(reason="256 two-byte values, one to a partition"):
             nc.scalar.dma_start(out=c_bf16[:], in_=c_norm2.rearrange("(a p) -> p a", p=P))
@@ -97,7 +97,6 @@ def tile_rbfnet_pb_k_kernel(
                 order.remove(order[0])
                 if kind == "s":
                     nc.sync.dma_start(out=s_row[0:1, :], in_=s_norm2.rearrange("(o n) -> o n", o=1))
-                    load_scales(nc.sync, I32, sm_planes[0], sM_scales[:GROUP])
                 elif kind == "x":
                     cols = slice(first * K_PASS, (first + count) * K_PASS)
                     for jt in range(TEST_TILES):

from contextlib import ExitStack

import concourse.mybir as mybir
from concourse.masks import make_identity

F32 = mybir.dt.float32
BF16 = mybir.dt.bfloat16
I32 = mybir.dt.int32
U32 = mybir.dt.uint32
U8 = mybir.dt.uint8
FP8X4 = mybir.dt.float8_e4m3fn_x4
ALU = mybir.AluOpType
ACT = mybir.ActivationFunctionType
AXIS = mybir.AxisListType

P = 128
PACK = 4
K_PASS = P * PACK
NTR, NTE, D, C = 2048, 256, 8192, 128
GAMMA = 10.0

FEAT_PASSES = D // K_PASS
TEST_TILES = NTE // P
BLOCK = 512
BLOCKS = NTR // BLOCK
HALF = BLOCK // 2
GROUP = 4
GROUPS = FEAT_PASSES // GROUP
QUADRANT = 32
SCALE_ROWS = 4
LIVE = GROUP * SCALE_ROWS
QUAD_ORDER = (0, 2, 1, 3)
WIDE = 2
STEP = 2
LOOKAHEAD = 6
WARM_START, WARM_BETWEEN, WARM_END = 6, 2, 16
SPLIT = 8
CHUNK = 4
X_PASSES = 8

FLOPS = 2 * NTR * D * NTE + 2 * NTE * NTR * C


def tile_rbfnet_pb_k_kernel(
    tc, sM_words, sM_scales, x_test, s_norm2, c_norm2, y_train_words, y_train_scales, out
):
    nc = tc.nc
    with ExitStack() as stack:
        keep = stack.enter_context(tc.tile_pool(name="keep", bufs=1))
        xstage = stack.enter_context(tc.tile_pool(name="xstage", bufs=2))
        stream = stack.enter_context(tc.tile_pool(name="stream", bufs=LOOKAHEAD + 2))
        narrow = stack.enter_context(tc.tile_pool(name="narrow", bufs=9))
        work = stack.enter_context(tc.tile_pool(name="work", bufs=4))
        psum_wide = stack.enter_context(tc.psum_pool(name="psum_wide", bufs=4))
        psum_turn = stack.enter_context(tc.psum_pool(name="psum_turn", bufs=4))
        stack.enter_context(tc.manual_schedule())

        sm_planes = []
        for a in range(GROUPS):
            plane = keep.tile([P, NTR], U8, align_bytes=256, name="sm_planes_%d" % a)
            sm_planes.append(plane)
        y_planes = keep.tile([P, C], U8, align_bytes=256)

        def load_scales(queue, dtype, plane, source):
            for quad in QUAD_ORDER:
                queue.dma_start(
                    out=plane[quad * QUADRANT : quad * QUADRANT + LIVE, :].bitcast(dtype),
                    in_=source[:, quad * SCALE_ROWS : (quad + 1) * SCALE_ROWS, :].bitcast(dtype),
                )

        nc.vector.memset(sm_planes[0][:].bitcast(I32), 0)
        ones = keep.tile([P, BLOCK], BF16)
        nc.vector.memset(ones[:], 1.0)
        s_row = keep.tile([P, NTR], BF16)
        nc.vector.memset(s_row[:].bitcast(I32), 0)
        ident_f32 = keep.tile([P, P], F32)
        make_identity(nc, ident_f32[:])
        for a in range(GROUPS):
            if a > 0:
                nc.vector.memset(sm_planes[a][:].bitcast(I32), 0)
            load_scales(nc.gpsimd, F32, sm_planes[a], sM_scales[a * GROUP : (a + 1) * GROUP])
        c_bf16 = keep.tile([P, TEST_TILES], BF16)
        with nc.allow_non_contiguous_dma(reason="256 two-byte values, one to a partition"):
            nc.scalar.dma_start(out=c_bf16[:], in_=c_norm2.rearrange("(a p) -> p a", p=P))
        nc.gpsimd.memset(y_planes[:].bitcast(I32), 0)
        ident_bf16 = keep.tile([P, P], BF16)
        make_identity(nc, ident_bf16[:])

        x_raw = keep.tile([P, TEST_TILES, D], BF16)
        sm_tiles = {}
        order = [("x", 0, X_PASSES), ("s", 0, 0), ("x", X_PASSES, X_PASSES)]
        order += [("m", g, 1) for g in range(FEAT_PASSES)]

        def issue(last_pass):
            while order and (order[0][0] != "m" or order[0][1] <= last_pass):
                kind, first, count = order[0]
                order.remove(order[0])
                if kind == "s":
                    nc.sync.dma_start(out=s_row[0:1, :], in_=s_norm2.rearrange("(o n) -> o n", o=1))
                elif kind == "x":
                    cols = slice(first * K_PASS, (first + count) * K_PASS)
                    for jt in range(TEST_TILES):
                        nc.sync.dma_start(
                            out=x_raw[:, jt, cols], in_=x_test[jt * P : (jt + 1) * P, cols]
                        )
                else:
                    sm_tiles[first] = stream.tile(
                        [P, WIDE * BLOCK], I32, align_bytes=256, tag="sm", name="sm_%d" % first
                    )
                    nc.sync.dma_start(
                        out=sm_tiles[first][:],
                        in_=sM_words[first, :, : WIDE * BLOCK, :]
                        .rearrange("p n t -> p (n t)")
                        .bitcast(I32),
                    )

        x_words = x_raw[:].bitcast(F32)
        x_codes = keep.tile([P, TEST_TILES, FEAT_PASSES, P], U32, align_bytes=256)
        x_planes = keep.tile([P, TEST_TILES, FEAT_PASSES, P], U8, align_bytes=256)
        half = K_PASS // 2

        runs, grouped = {}, {}

        def reorder(jt, first):
            runs[jt, first] = xstage.tile([P, X_PASSES, 2, P], F32, tag="runs", name="runs")
            nc.vector.tensor_copy(
                out=runs[jt, first][:],
                in_=x_words[:, jt, first * half : (first + X_PASSES) * half].rearrange(
                    "j (g p u) -> j g u p", g=X_PASSES, u=2
                ),
            )

        def turn_words(jt, first):
            grouped[jt, first] = xstage.tile(
                [P, X_PASSES, P, PACK], BF16, align_bytes=256, tag="grouped", name="grouped"
            )
            grouped_words = grouped[jt, first][:].bitcast(F32)
            for i in range(0, X_PASSES, 2):
                xt = psum_turn.tile([P, 2, 2, P], F32, tag="turn", name="xt")
                for g in range(2):
                    for u in range(2):
                        nc.tensor.transpose(xt[:, g, u, :], runs[jt, first][:, i + g, u, :], ident_f32[:])
                copy = nc.vector.tensor_copy if i == X_PASSES - 2 else nc.scalar.copy
                copy(
                    out=grouped_words[:, i : i + 2], in_=xt[:].rearrange("p g u j -> p g j u")
                )

        def quantise_words(jt, first):
            passes = slice(first, first + X_PASSES)
            nc.vector.quantize_mx(
                out=x_codes[:, jt, passes, :].rearrange("p g j -> p (g j)").bitcast(FP8X4),
                scales=x_planes[:, jt, passes, :].rearrange("p g j -> p (g j)"),
                in_=grouped[jt, first][:].rearrange("p g j t -> p (g j t)"),
            )

        kern = keep.tile([P, TEST_TILES, BLOCKS, PACK, P], F32)
        ksum = keep.tile([P, TEST_TILES, BLOCKS], F32)
        last_d2 = keep.tile([P, TEST_TILES, PACK, P], F32)
        s_all = keep.tile([P, BLOCKS, PACK, P], BF16)
        c_col = keep.tile([P, TEST_TILES], F32)
        acc, d2 = {}, {}

        def multiply(g, words, unit):
            jt, n0, n = unit
            a, b = divmod(g, GROUP)
            nc.tensor.matmul_mx(
                out=acc[unit][:],
                lhsT=x_codes[:, jt, g, :].bitcast(FP8X4),
                lhsT_scale=x_planes[:, jt, g, :],
                rhs=words.bitcast(FP8X4),
                rhs_scale=sm_planes[a][b * SCALE_ROWS : P, n0 : n0 + n],
                start=(g == 0),
                stop=(g == FEAT_PASSES - 1),
            )

        def place(tensor, unit):
            jt, n0, n = unit
            q0 = n0 % BLOCK // PACK
            return tensor[:, :, q0 : q0 + n // PACK]

        def squared_distance(unit):
            jt, n0, n = unit
            if n == BLOCK:
                whole = work.tile([P, PACK, P], F32, tag="d2", name="d2")
                d2[unit] = whole[:]
            else:
                d2[unit] = place(last_d2[:, jt], unit)
            nc.vector.scalar_tensor_tensor(
                out=d2[unit],
                in0=acc[unit][:].rearrange("p (q t) -> p t q", t=PACK),
                scalar=-2.0,
                in1=place(s_all[:, n0 // BLOCK], unit),
                op0=ALU.mult,
                op1=ALU.add,
            )
            nc.vector.tensor_scalar(
                out=d2[unit], in0=d2[unit],
                scalar1=c_col[:, jt : jt + 1], scalar2=0.0, op0=ALU.add, op1=ALU.max,
            )

        def root(unit):
            nc.scalar.activation(out=d2[unit], in_=d2[unit], func=ACT.Sqrt)

        def exponential(jt, blk, source):
            nc.scalar.activation(
                out=kern[:, jt, blk], in_=source, func=ACT.Exp,
                scale=-1.0 / GAMMA, accum_out=ksum[:, jt, blk : blk + 1],
            )

        spare = keep.tile([P, 1], F32)

        def load_root_table():
            nc.scalar.activation(out=spare[:], in_=ksum[:, 0, 0:1], func=ACT.Sqrt)

        def open_banks(pool, tag, units):
            for unit in units:
                acc[unit] = pool.tile([P, unit[2]], F32, tag=tag, name="acc_%d_%d" % unit[:2])

        def narrow_load(pool, tag, first, passes, n0, n):
            sm = pool.tile([P, passes, n], I32, align_bytes=256, tag=tag, name="sm")
            nc.sync.dma_start(
                out=sm[:],
                in_=sM_words[first : first + passes, :, n0 : n0 + n, :]
                .rearrange("g p n t -> p g (n t)")
                .bitcast(I32),
            )
            return sm

        def spread_s_norm2():
            for blk in range(BLOCKS):
                s_bank = psum_turn.tile([P, BLOCK], F32, tag="turn", name="s_bank")
                nc.tensor.matmul(
                    out=s_bank[:], lhsT=ones[:, :P], rhs=s_row[:, blk * BLOCK : (blk + 1) * BLOCK],
                    start=True, stop=True,
                )
                nc.scalar.copy(out=s_all[:, blk], in_=s_bank[:].rearrange("p (q t) -> p t q", t=PACK))

        issue(LOOKAHEAD)

        def keep_warm(count):
            warm = psum_wide.tile([P, BLOCK], F32, tag="wide", name="warm")
            for i in range(count):
                nc.tensor.matmul(out=warm[:], lhsT=ones[:, :P], rhs=ones[:], start=True, stop=True)

        keep_warm(WARM_START)
        x_pieces = [(jt, first) for first in range(0, FEAT_PASSES, X_PASSES) for jt in range(TEST_TILES)]
        reorder(*x_pieces[0])
        reorder(*x_pieces[1])

        def make_ready(n):
            turn_words(*x_pieces[n])
            quantise_words(*x_pieces[n])
            if n + 2 < len(x_pieces):
                reorder(*x_pieces[n + 2])

        make_ready(0)
        keep_warm(WARM_BETWEEN)
        make_ready(1)
        spread_s_norm2()
        make_ready(2)

        first_units = [(jt, blk * BLOCK, BLOCK) for jt in range(TEST_TILES) for blk in range(WIDE)]
        open_banks(psum_wide, "wide", first_units)
        for g in range(FEAT_PASSES):
            issue(g + LOOKAHEAD)
            if g == 3:
                make_ready(3)
                nc.vector.tensor_copy(out=c_col[:], in_=c_bf16[:])
            for unit in first_units:
                multiply(g, sm_tiles[g][:, unit[1] : unit[1] + BLOCK], unit)

        n0 = WIDE * BLOCK
        second_units = [(jt, n0, BLOCK) for jt in range(TEST_TILES)]
        tiles = [narrow_load(narrow, "sm", first, STEP, n0, BLOCK) for first in range(0, FEAT_PASSES, STEP)]
        open_banks(psum_turn, "turn", second_units)
        for first in range(0, FEAT_PASSES, STEP):
            for unit in second_units:
                for i in range(STEP):
                    multiply(first + i, tiles[first // STEP][:, i, :], unit)
        for unit in first_units:
            squared_distance(unit)
        for unit in first_units:
            root(unit)
        for unit in first_units:
            exponential(unit[0], unit[1] // BLOCK, d2[unit])
        load_root_table()

        n0 = (BLOCKS - 1) * BLOCK
        left_units = [(jt, n0, HALF) for jt in range(TEST_TILES)]
        right_units = [(jt, n0 + HALF, HALF) for jt in range(TEST_TILES)]
        tiles = [narrow_load(narrow, "sm", first, STEP, n0, BLOCK) for first in range(0, SPLIT, STEP)]
        ends = [
            [narrow_load(keep, "end_%d_%d" % (h, first), first, CHUNK, n0 + h * HALF, HALF)
             for first in range(SPLIT, FEAT_PASSES, CHUNK)]
            for h in range(2)
        ]
        load_scales(nc.sync, I32, y_planes, y_train_scales)
        y_codes = keep.tile([P, BLOCKS, C], I32, align_bytes=256)
        nc.sync.dma_start(
            out=y_codes[:], in_=y_train_words.rearrange("g p n t -> p g (n t)").bitcast(I32)
        )
        open_banks(psum_wide, "wide", left_units)
        open_banks(psum_wide, "wide", right_units)
        for g in range(SPLIT):
            for jt in range(TEST_TILES):
                multiply(g, tiles[g // STEP][:, g % STEP, :HALF], left_units[jt])
                multiply(g, tiles[g // STEP][:, g % STEP, HALF:], right_units[jt])
        for unit in second_units:
            squared_distance(unit)
        for unit in second_units:
            root(unit)
        for unit in second_units:
            exponential(unit[0], unit[1] // BLOCK, d2[unit])
        load_root_table()
        for words, units in zip(ends, (left_units, right_units)):
            for first in range(SPLIT, FEAT_PASSES, CHUNK):
                for unit in units:
                    for i in range(CHUNK):
                        multiply(first + i, words[(first - SPLIT) // CHUNK][:, i, :], unit)
            for unit in units:
                squared_distance(unit)
            for unit in units:
                root(unit)
        for jt in range(TEST_TILES):
            exponential(jt, BLOCKS - 1, last_d2[:, jt])
        keep_warm(WARM_END)

        total = keep.tile([P, TEST_TILES], F32)
        rsum = keep.tile([P, TEST_TILES], F32)
        w_codes = keep.tile([P, TEST_TILES, BLOCKS, P], U32, align_bytes=256)
        w_planes = keep.tile([P, TEST_TILES, BLOCKS, P], U8, align_bytes=256)
        pieces = [(jt, blk) for jt in range(TEST_TILES) for blk in range(BLOCKS)]
        on_scalar = (1, 0)
        w_bf16, w_grouped, o_bank = {}, {}, {}

        def reciprocal_sum(jt):
            nc.vector.tensor_reduce(
                out=total[:, jt : jt + 1], in_=ksum[:, jt, :], axis=AXIS.X, op=ALU.add
            )
            nc.vector.reciprocal(out=rsum[:, jt : jt + 1], in_=total[:, jt : jt + 1])

        def normalise(piece):
            jt, blk = piece
            w_bf16[piece] = work.tile([P, PACK, P], BF16, tag="w_bf16", name="w_bf16")
            if piece == on_scalar:
                nc.scalar.activation(
                    out=w_bf16[piece][:], in_=kern[:, jt, blk], func=ACT.Copy, scale=rsum[:, jt : jt + 1]
                )
            else:
                nc.vector.tensor_scalar(
                    out=w_bf16[piece][:], in0=kern[:, jt, blk], scalar1=rsum[:, jt : jt + 1],
                    scalar2=None, op0=ALU.mult,
                )

        def turn(piece):
            wt = psum_wide.tile([P, PACK, P], BF16, tag="wide", name="wt")
            for t in range(PACK):
                nc.tensor.transpose(wt[:, t, :], w_bf16[piece][:, t, :], ident_bf16[:])
            jt, blk = piece
            if blk % 2 == 0:
                w_grouped[jt, blk // 2] = work.tile(
                    [P, 2, P, PACK], BF16, align_bytes=256, tag="w_grouped", name="w_grouped"
                )
            nc.scalar.copy(
                out=w_grouped[jt, blk // 2][:, blk % 2], in_=wt[:].rearrange("p t j -> p j t")
            )

        def quantise(jt, first, count):
            half, inner = divmod(first, 2)
            blocks = slice(first, first + count)
            nc.vector.quantize_mx(
                out=w_codes[:, jt, blocks, :].rearrange("p b j -> p (b j)").bitcast(FP8X4),
                scales=w_planes[:, jt, blocks, :].rearrange("p b j -> p (b j)"),
                in_=w_grouped[jt, half][:, inner : inner + count].rearrange("p b j t -> p (b j t)"),
            )

        def second_product(piece):
            jt, blk = piece
            if blk == 0:
                o_bank[jt] = psum_turn.tile([P, C], F32, tag="turn", name="o_bank")
            nc.tensor.matmul_mx(
                out=o_bank[jt][:],
                lhsT=w_codes[:, jt, blk, :].bitcast(FP8X4),
                lhsT_scale=w_planes[:, jt, blk, :],
                rhs=y_codes[:, blk, :].bitcast(FP8X4),
                rhs_scale=y_planes[blk * SCALE_ROWS : P, :],
                start=(blk == 0),
                stop=(blk == BLOCKS - 1),
            )
            if blk == BLOCKS - 1:
                result = work.tile([P, C], F32, name="result")
                copy = nc.scalar.copy if jt == 0 else nc.vector.tensor_copy
                copy(out=result[:], in_=o_bank[jt][:])
                nc.sync.dma_start(out=out[jt * P : (jt + 1) * P, :], in_=result[:])

        reciprocal_sum(0)
        for n, piece in enumerate(pieces):
            if n == 1:
                reciprocal_sum(1)
            if n == 2:
                normalise(on_scalar)
            if piece != on_scalar:
                normalise(piece)
            turn(piece)
            if n == BLOCKS - 1:
                quantise(0, 0, 2)
        quantise(0, 2, 2)
        quantise(1, 0, 2)
        for piece in pieces[:BLOCKS]:
            second_product(piece)
        for piece in pieces[BLOCKS:]:
            if piece[1] >= 2:
                quantise(*piece, 1)
            second_product(piece)
